import numpy as np
import ml_dtypes


def mxq(x, axis, fmt="e4m3"):
    dtype, down = {"e4m3": (ml_dtypes.float8_e4m3fn, 7), "e5m2": (ml_dtypes.float8_e5m2, 14)}[fmt]
    v = np.moveaxis(np.asarray(x, np.float32).astype(ml_dtypes.bfloat16).astype(np.float64), axis, -1)
    blocks = v.reshape(v.shape[:-1] + (-1, 32))
    amax = np.abs(blocks).max(-1, keepdims=True)
    byte = np.maximum(np.where(amax > 0, np.frexp(amax)[1] - 1 + 127, 0) - down, 1)
    scale = np.exp2(byte - 127.0)
    codes = (blocks / scale).astype(np.float32).astype(dtype).astype(np.float64)
    return np.moveaxis((codes * scale).reshape(v.shape), -1, axis)


WIDE = False


def mx_kscale(k):
    if not WIDE:
        return np.ones(k)
    levels = np.array([10, -10, 5, -5, 0])
    a = np.random.permutation(np.resize(levels, k // 512 * 4)).reshape(k // 512, 4)
    idx = np.arange(k)
    return np.exp2(a[idx // 512, idx % 128 // 32])


BF16 = ml_dtypes.bfloat16


def bf(x):
    return np.asarray(x, np.float32).astype(BF16)


def f64(x):
    return np.asarray(x).astype(np.float64)


E2M1 = np.array([0.0, 0.5, 1.0, 1.5, 2.0, 3.0, 4.0, 6.0, -0.0, -0.5, -1.0, -1.5, -2.0, -3.0, -4.0, -6.0])


def pack_weight(w, fmt):
    k, n = w.shape
    w = f64(bf(w)).reshape(k // 32, 32, n)
    amax = np.abs(w).max(1)
    if fmt == "e4m3":
        byte = np.frexp(amax)[1] - 1 + 127 - 7
    else:
        mant, ex = np.frexp(amax / 6.0)
        byte = np.where(mant > 0.5, ex, ex - 1) + 127
    byte = np.clip(np.where(amax > 0, byte, 1), 1, 254)
    scaled = (w * np.exp2(127.0 - byte)[:, None, :]).reshape(k, n).astype(np.float32)
    by_word = np.ascontiguousarray(scaled.reshape(k // 512, 128, 4, n).transpose(0, 1, 3, 2))
    if fmt == "e4m3":
        words = by_word.astype(ml_dtypes.float8_e4m3fn).view(np.uint8)
    else:
        c = by_word.astype(ml_dtypes.float4_e2m1fn).view(np.uint8) & 0xF
        words = c[..., 0::2] | (c[..., 1::2] << 4)
    return np.ascontiguousarray(words), np.ascontiguousarray(byte.astype(np.uint8).reshape(k // 512, 16, n))


def unpack_weight(words, scales, fmt):
    g, p, n, _ = words.shape
    if fmt == "e4m3":
        vals = np.ascontiguousarray(words).view(ml_dtypes.float8_e4m3fn).astype(np.float64)
    else:
        nib = np.empty((g, p, n, 4), np.uint8)
        nib[..., 0::2] = words & 0xF
        nib[..., 1::2] = words >> 4
        vals = E2M1[nib]
    vals = vals * np.repeat(np.exp2(scales.astype(np.float64) - 127.0), 8, axis=1)[..., None]
    return vals.transpose(0, 1, 3, 2).reshape(g * 512, n)


B, N, F, U, S = 2, 512, 3584, 512, 2
C = S * (F + U)
FMT = "e4m3"


def sigmoid(v):
    return 1.0 / (1.0 + np.exp(-v))


def random_walk():
    a = np.random.uniform(size=(N, N))
    return a / a.sum(axis=1, keepdims=True) * np.sqrt(N)


def setup_inputs():
    s = mx_kscale(N)
    r_prev = bf(sigmoid(np.random.standard_normal((B, U, N))) * np.random.standard_normal((B, U, N)) * s)
    h_diff = bf(np.random.standard_normal((B, N, S * F)))
    u = bf(sigmoid(np.random.standard_normal((B, N, U))))
    state = bf(np.random.standard_normal((B, U * N)))
    s0_words, s0_scales = pack_weight(np.ascontiguousarray((random_walk() / s[None, :]).T), FMT)
    s1_words, s1_scales = pack_weight(np.ascontiguousarray((random_walk() / s[None, :]).T), FMT)
    ck_words, ck_scales = pack_weight(np.random.standard_normal((C, U)) / np.sqrt(C), FMT)
    return {"r_prev": r_prev,
            "h_diff": h_diff,
            "u": u,
            "state": state,
            "support0_words": s0_words,
            "support0_scales": s0_scales,
            "support1_words": s1_words,
            "support1_scales": s1_scales,
            "c_kernel_words": ck_words,
            "c_kernel_scales": ck_scales}


def diffuse(xq, supq):
    return np.concatenate([(xq @ sq.T) for sq in supq], axis=1)


def reference(r_prev, h_diff, u, state, support0_words, support0_scales, support1_words, support1_scales, c_kernel_words, c_kernel_scales):
    supq = (unpack_weight(support0_words, support0_scales, FMT).T, unpack_weight(support1_words, support1_scales, FMT).T)
    c_state = diffuse(mxq(f64(r_prev), 2, "e4m3"), supq).transpose(0, 2, 1)
    hc = np.concatenate([f64(h_diff), c_state], axis=-1)
    c = np.tanh(mxq(hc, 2, "e4m3") @ unpack_weight(c_kernel_words, c_kernel_scales, FMT))
    prev_t = f64(state).reshape(B, U, N).transpose(0, 2, 1)
    ug = f64(u)
    z = ug * prev_t + (1.0 - ug) * c
    return z.reshape(B, U * N)

@@ -1,0 +1,302 @@
+from contextlib import ExitStack
+
+import concourse.mybir as mybir
+from concourse.masks import make_identity
+
+F32 = mybir.dt.float32
+BF16 = mybir.dt.bfloat16
+I32 = mybir.dt.int32
+U32 = mybir.dt.uint32
+U8 = mybir.dt.uint8
+FP8X4 = mybir.dt.float8_e4m3fn_x4
+TANH = mybir.ActivationFunctionType.Tanh
+
+P = 128
+PACK = 4
+K_PASS = P * PACK
+WORDS_PER_PASS = K_PASS // 2
+
+BATCH = 2
+NODES = 512
+UNITS = 512
+SUPPORTS = 2
+H_CHANNELS = 7168
+BLOCKS_PER_BATCH = NODES // P
+ROW_BLOCKS = BATCH * BLOCKS_PER_BATCH
+H_PASSES = H_CHANNELS // K_PASS
+ALL_PASSES = H_PASSES + SUPPORTS
+ROUND_PASSES = 8
+ROUND_COLS = ROUND_PASSES * K_PASS
+SCALE_ROWS = K_PASS // 32
+
+ROUNDS = [(2 * pair + k, half) for pair in range(ROW_BLOCKS // 2) for half in range(2) for k in range(2)]
+SORT_AHEAD = 3
+RAW_BUFS = 5
+LOAD_AHEAD = SORT_AHEAD + RAW_BUFS - 1
+
+FLOPS = 2 * (BATCH * SUPPORTS * UNITS * NODES * NODES + BATCH * NODES * (H_CHANNELS + SUPPORTS * UNITS) * UNITS)
+
+
+def tile_gcrnncell_pb_k_kernel(
+    tc,
+    r_prev,
+    h_diff,
+    u,
+    state,
+    support0_words,
+    support0_scales,
+    support1_words,
+    support1_scales,
+    c_kernel_words,
+    c_kernel_scales,
+    out,
+):
+    nc = tc.nc
+    h_rows = h_diff.flatten_outer_dims()
+    u_rows = u.flatten_outer_dims()
+    out_rows = out.rearrange("b (n k) -> (b n) k", k=UNITS)
+    support_words = (support0_words, support1_words)
+    support_scales = (support0_scales, support1_scales)
+
+    with ExitStack() as ctx:
+        keep = ctx.enter_context(tc.tile_pool(name="keep", bufs=1))
+        raw_pool = ctx.enter_context(tc.tile_pool(name="raw", bufs=RAW_BUFS))
+        sorted_pool = ctx.enter_context(tc.tile_pool(name="sorted", bufs=3))
+        grouped_pool = ctx.enter_context(tc.tile_pool(name="grouped", bufs=3))
+        codes_pool = ctx.enter_context(tc.tile_pool(name="codes", bufs=3))
+        diffused_pool = ctx.enter_context(tc.tile_pool(name="diffused", bufs=2))
+        blend_pool = ctx.enter_context(tc.tile_pool(name="blend", bufs=2))
+        ring = ctx.enter_context(tc.psum_pool(name="ring", bufs=6))
+        acc_pool = ctx.enter_context(tc.psum_pool(name="acc", bufs=2))
+        ctx.enter_context(tc.manual_schedule())
+
+        ident_f32 = keep.tile([P, P], F32)
+        ident_bf16 = keep.tile([P, P], BF16)
+        table_warmer = keep.tile([P, 1], F32)
+        kernel_words = keep.tile([P, ALL_PASSES, UNITS], U32, align_bytes=64)
+        kernel_planes = keep.tile([P, ALL_PASSES, UNITS], U8, align_bytes=64)
+        sup_words = keep.tile([P, SUPPORTS, NODES], U32, align_bytes=64)
+        sup_planes = keep.tile([P, SUPPORTS, NODES], U8, align_bytes=64)
+        cs_codes = keep.tile([P, SUPPORTS, ROW_BLOCKS, P], U32, align_bytes=64)
+        cs_planes = keep.tile([P, SUPPORTS, ROW_BLOCKS, P], U8, align_bytes=64)
+        u_sb = keep.tile([P, ROW_BLOCKS, UNITS], BF16)
+        state_sb = keep.tile([P, BATCH, UNITS // P, NODES], BF16)
+
+        raw_of = {}
+        sorted_of = {}
+        banks_of = {}
+        prev_bank_of = {}
+        operand_of = {}
+        prev_of = {}
+        acc_of = {}
+
+        def h_passes_of(half):
+            return ROUND_PASSES if half == 0 else H_PASSES - ROUND_PASSES
+
+        def load_round(i):
+            row_block, half = ROUNDS[i]
+            width = h_passes_of(half) * K_PASS
+            first = half * ROUND_COLS
+            raw = raw_pool.tile([P, ROUND_COLS], BF16)
+            nc.sync.dma_start(
+                out=raw[:, :width],
+                in_=h_rows[row_block * P : (row_block + 1) * P, first : first + width],
+            )
+            raw_of[i] = raw
+
+        def sort_words(raw, srt, first_pass, n_passes):
+            words = raw[:, first_pass * K_PASS : (first_pass + n_passes) * K_PASS].bitcast(F32)
+            nc.vector.tensor_copy(
+                out=srt[:, first_pass : first_pass + n_passes],
+                in_=words.rearrange("p (g j e) -> p g e j", j=P, e=2),
+            )
+
+        def sort_round(i):
+            srt = sorted_pool.tile([P, ROUND_PASSES, 2, P], F32)
+            sort_words(raw_of[i], srt, 0, h_passes_of(ROUNDS[i][1]))
+            sorted_of[i] = srt
+
+        def transpose_passes(srt, n_passes):
+            banks = []
+            for pair in range(n_passes // 2):
+                bank = ring.tile([P, 2, 2, P], F32, tag="ring")
+                for g in range(2):
+                    for parity in range(2):
+                        nc.tensor.transpose(bank[:, g, parity, :], srt[:, 2 * pair + g, parity, :], ident_f32[:])
+                banks.append(bank)
+            return banks
+
+        def transpose_round(i):
+            row_block, half = ROUNDS[i]
+            banks_of[i] = transpose_passes(sorted_of[i], h_passes_of(half))
+            if half == 1:
+                b, node_block = divmod(row_block, BLOCKS_PER_BATCH)
+                prev_bank = ring.tile([P, UNITS], BF16, tag="ring")
+                for unit_block in range(UNITS // P):
+                    nc.tensor.transpose(
+                        prev_bank[:, unit_block * P : (unit_block + 1) * P],
+                        state_sb[:, b, unit_block, node_block * P : (node_block + 1) * P],
+                        ident_bf16[:],
+                    )
+                prev_bank_of[i] = prev_bank
+
+        def quantise_banks(banks):
+            grouped = grouped_pool.tile([P, ROUND_PASSES, P, PACK], BF16, align_bytes=64)
+            codes = codes_pool.tile([P, ROUND_PASSES, P], U32, align_bytes=64)
+            planes = codes_pool.tile([P, ROUND_PASSES, P], U8, align_bytes=64)
+            for pair, bank in enumerate(banks):
+                two = slice(2 * pair, 2 * pair + 2)
+                nc.scalar.copy(out=grouped[:, two].bitcast(F32), in_=bank[:].rearrange("p g e r -> p g r e"))
+                nc.vector.quantize_mx(
+                    out=codes[:, two, :].rearrange("p g r -> p (g r)").bitcast(FP8X4),
+                    scales=planes[:, two, :].rearrange("p g r -> p (g r)"),
+                    in_=grouped[:, two].rearrange("p g r t -> p (g r t)"),
+                )
+            return codes, planes
+
+        def quantise_round(i):
+            operand_of[i] = quantise_banks(banks_of[i])
+            if ROUNDS[i][1] == 1:
+                prev = blend_pool.tile([P, UNITS], BF16)
+                nc.scalar.copy(out=prev[:], in_=prev_bank_of[i][:])
+                prev_of[ROUNDS[i][0]] = prev
+
+        def kernel_pass(acc, codes, planes, g):
+            nc.tensor.matmul_mx(
+                out=acc[:],
+                lhsT=codes.bitcast(FP8X4),
+                lhsT_scale=planes,
+                rhs=kernel_words[:, g, :].bitcast(FP8X4),
+                rhs_scale=kernel_planes[:, g, :],
+                start=(g == 0),
+                stop=(g == ALL_PASSES - 1),
+            )
+
+        def passes_of_round(i):
+            row_block, half = ROUNDS[i]
+            if half == 0:
+                acc = acc_pool.tile([P, UNITS], F32)
+                acc_of[row_block] = acc
+            acc = acc_of[row_block]
+            codes, planes = operand_of[i]
+            for g in range(h_passes_of(half)):
+                kernel_pass(acc, codes[:, g, :], planes[:, g, :], half * ROUND_PASSES + g)
+            if half == 1:
+                for s in range(SUPPORTS):
+                    kernel_pass(acc, cs_codes[:, s, row_block, :], cs_planes[:, s, row_block, :], H_PASSES + s)
+
+        def blend(row_block):
+            cand = blend_pool.tile([P, UNITS], F32)
+            nc.scalar.activation(out=cand[:], in_=acc_of[row_block][:], func=TANH)
+            diff = blend_pool.tile([P, UNITS], F32)
+            nc.vector.tensor_sub(out=diff[:], in0=prev_of[row_block][:], in1=cand[:])
+            nc.vector.tensor_mul(out=diff[:], in0=diff[:], in1=u_sb[:, row_block, :])
+            z = blend_pool.tile([P, UNITS], F32)
+            nc.vector.tensor_add(out=z[:], in0=diff[:], in1=cand[:])
+            nc.sync.dma_start(out=out_rows[row_block * P : (row_block + 1) * P, :], in_=z[:])
+
+        def diffuse(b, r_codes, r_planes):
+            for s in range(SUPPORTS):
+                diffused = diffused_pool.tile([P, BLOCKS_PER_BATCH, P, PACK], BF16, align_bytes=64)
+                for node_block in range(BLOCKS_PER_BATCH):
+                    nodes = slice(node_block * P, (node_block + 1) * P)
+                    bank = ring.tile([P, PACK, P], F32, tag="ring")
+                    for t in range(PACK):
+                        nc.tensor.matmul_mx(
+                            out=bank[:, t, :],
+                            lhsT=r_codes[:, PACK * b + t, :].bitcast(FP8X4),
+                            lhsT_scale=r_planes[:, PACK * b + t, :],
+                            rhs=sup_words[:, s, nodes].bitcast(FP8X4),
+                            rhs_scale=sup_planes[:, s, nodes],
+                            start=True,
+                            stop=True,
+                        )
+                    by_unit = bank[:].rearrange("p t m -> p m t")
+                    if node_block % 2 == 0:
+                        nc.scalar.copy(out=diffused[:, node_block], in_=by_unit)
+                    else:
+                        nc.vector.tensor_copy(out=diffused[:, node_block], in_=by_unit)
+                blocks = slice(b * BLOCKS_PER_BATCH, (b + 1) * BLOCKS_PER_BATCH)
+                nc.vector.quantize_mx(
+                    out=cs_codes[:, s, blocks, :].rearrange("p r m -> p (r m)").bitcast(FP8X4),
+                    scales=cs_planes[:, s, blocks, :].rearrange("p r m -> p (r m)"),
+                    in_=diffused[:].rearrange("p r m t -> p (r m t)"),
+                )
+
+        def load_kernel_words(first, count):
+            nc.sync.dma_start(
+                out=kernel_words[:, first : first + count, :].bitcast(I32),
+                in_=c_kernel_words[first : first + count].rearrange("g p n t -> p g (n t)").bitcast(I32),
+            )
+
+        def load_state(b):
+            nc.sync.dma_start(out=state_sb[:, b], in_=state[b].rearrange("(c p n) -> p c n", p=P, n=NODES))
+
+        nc.vector.memset(sup_planes[:].rearrange("p s n -> p (s n)").bitcast(I32), 0)
+        nc.vector.memset(kernel_planes[:].rearrange("p g n -> p (g n)").bitcast(I32), 0)
+        nc.vector.memset(table_warmer[:], 0.0)
+        nc.scalar.activation(out=table_warmer[:], in_=table_warmer[:], func=TANH)
+        make_identity(nc, ident_f32[:])
+        make_identity(nc, ident_bf16[:])
+
+        r_raw = raw_pool.tile([P, ROUND_COLS], BF16, tag="raw")
+        for b in range(BATCH):
+            nc.sync.dma_start(
+                out=r_raw[:, b * PACK * NODES : (b + 1) * PACK * NODES],
+                in_=r_prev[b].rearrange("(p t) n -> p (t n)", t=PACK),
+            )
+        for s in range(SUPPORTS):
+            nc.sync.dma_start(
+                out=sup_words[:, s, :].bitcast(I32),
+                in_=support_words[s][0].rearrange("p n t -> p (n t)").bitcast(I32),
+            )
+        for s in range(SUPPORTS):
+            for r in range(4):
+                nc.sync.dma_start(
+                    out=sup_planes[r:P:32, s, :].bitcast(I32),
+                    in_=support_scales[s][0, r:SCALE_ROWS:4, :].bitcast(I32),
+                )
+        load_round(0)
+        load_round(1)
+        for r in range(4):
+            nc.sync.dma_start(
+                out=kernel_planes[r:P:32, :, :].bitcast(I32),
+                in_=c_kernel_scales[:, r:SCALE_ROWS:4, :].rearrange("g q n -> q g n").bitcast(I32),
+            )
+        load_kernel_words(0, 4)
+        load_kernel_words(4, 4)
+        load_round(2)
+        load_state(0)
+        load_round(3)
+        load_kernel_words(8, 4)
+        load_kernel_words(12, 4)
+        nc.sync.dma_start(out=u_sb[:], in_=u_rows.rearrange("(r p) k -> p r k", p=P))
+
+        r_sorted = sorted_pool.tile([P, ROUND_PASSES, 2, P], F32, tag="srt")
+        for b in range(BATCH):
+            sort_words(r_raw, r_sorted, b * PACK, PACK)
+        load_round(4)
+        r_codes, r_planes = quantise_banks(transpose_passes(r_sorted, ROUND_PASSES))
+        sort_round(0)
+        load_round(5)
+        load_state(1)
+        diffuse(0, r_codes, r_planes)
+        transpose_round(0)
+        quantise_round(0)
+        sort_round(1)
+        load_round(6)
+        diffuse(1, r_codes, r_planes)
+        sort_round(2)
+
+        for i in range(len(ROUNDS)):
+            if i >= 1 and ROUNDS[i - 1][1] == 1:
+                blend(ROUNDS[i - 1][0])
+            if i + LOAD_AHEAD < len(ROUNDS):
+                load_round(i + LOAD_AHEAD)
+            if i + SORT_AHEAD < len(ROUNDS):
+                sort_round(i + SORT_AHEAD)
+            if i + 1 < len(ROUNDS):
+                transpose_round(i + 1)
+                quantise_round(i + 1)
+            passes_of_round(i)
+        blend(ROUNDS[-1][0])

@@ -31,8 +31,8 @@ SCALE_ROWS = K_PASS // 32
 
 ROUNDS = [(2 * pair + k, half) for pair in range(ROW_BLOCKS // 2) for half in range(2) for k in range(2)]
 SORT_AHEAD = 3
-RAW_BUFS = 5
-LOAD_AHEAD = SORT_AHEAD + RAW_BUFS - 1
+RAW_BUFS = 6
+LOAD_AHEAD = RAW_BUFS + 1
 
 FLOPS = 2 * (BATCH * SUPPORTS * UNITS * NODES * NODES + BATCH * NODES * (H_CHANNELS + SUPPORTS * UNITS) * UNITS)
 
@@ -113,22 +113,32 @@ def tile_gcrnncell_pb_k_kernel(
 
         def sort_round(i):
             srt = sorted_pool.tile([P, ROUND_PASSES, 2, P], F32)
-            sort_words(raw_of[i], srt, 0, h_passes_of(ROUNDS[i][1]))
+            sort_words(raw_of[i], srt, 0, ROUND_PASSES)
             sorted_of[i] = srt
 
-        def transpose_passes(srt, n_passes):
+        def transpose_passes(words_of, n_passes):
             banks = []
             for pair in range(n_passes // 2):
                 bank = ring.tile([P, 2, 2, P], F32, tag="ring")
                 for g in range(2):
                     for parity in range(2):
-                        nc.tensor.transpose(bank[:, g, parity, :], srt[:, 2 * pair + g, parity, :], ident_f32[:])
+                        nc.tensor.transpose(bank[:, g, parity, :], words_of(2 * pair + g, parity), ident_f32[:])
                 banks.append(bank)
             return banks
 
+        def sorted_words(srt):
+            return lambda g, parity: srt[:, g, parity, :]
+
+        def every_second_word(raw):
+            words = raw[:].bitcast(F32)
+            return lambda g, parity: words[:, g * WORDS_PER_PASS + parity : (g + 1) * WORDS_PER_PASS : 2]
+
         def transpose_round(i):
             row_block, half = ROUNDS[i]
-            banks_of[i] = transpose_passes(sorted_of[i], h_passes_of(half))
+            if half == 0:
+                banks_of[i] = transpose_passes(sorted_words(sorted_of[i]), ROUND_PASSES)
+            else:
+                banks_of[i] = transpose_passes(every_second_word(raw_of[i]), H_PASSES - ROUND_PASSES)
             if half == 1:
                 b, node_block = divmod(row_block, BLOCKS_PER_BATCH)
                 prev_bank = ring.tile([P, UNITS], BF16, tag="ring")
@@ -188,11 +198,16 @@ def tile_gcrnncell_pb_k_kernel(
         def blend(row_block):
             cand = blend_pool.tile([P, UNITS], F32)
             nc.scalar.activation(out=cand[:], in_=acc_of[row_block][:], func=TANH)
+            prev = prev_of[row_block]
             diff = blend_pool.tile([P, UNITS], F32)
-            nc.vector.tensor_sub(out=diff[:], in0=prev_of[row_block][:], in1=cand[:])
-            nc.vector.tensor_mul(out=diff[:], in0=diff[:], in1=u_sb[:, row_block, :])
             z = blend_pool.tile([P, UNITS], F32)
-            nc.vector.tensor_add(out=z[:], in0=diff[:], in1=cand[:])
+            halves = (slice(0, UNITS // 2), slice(UNITS // 2, UNITS))
+            for cols in halves:
+                nc.vector.tensor_sub(out=diff[:, cols], in0=prev[:, cols], in1=cand[:, cols])
+            for cols in halves:
+                nc.vector.tensor_mul(out=diff[:, cols], in0=diff[:, cols], in1=u_sb[:, row_block, cols])
+            for cols in halves:
+                nc.vector.tensor_add(out=z[:, cols], in0=diff[:, cols], in1=cand[:, cols])
             nc.sync.dma_start(out=out_rows[row_block * P : (row_block + 1) * P, :], in_=z[:])
 
         def diffuse(b, r_codes, r_planes):
@@ -271,32 +286,31 @@ def tile_gcrnncell_pb_k_kernel(
         load_kernel_words(8, 4)
         load_kernel_words(12, 4)
         nc.sync.dma_start(out=u_sb[:], in_=u_rows.rearrange("(r p) k -> p r k", p=P))
+        load_round(4)
 
         r_sorted = sorted_pool.tile([P, ROUND_PASSES, 2, P], F32, tag="srt")
         for b in range(BATCH):
             sort_words(r_raw, r_sorted, b * PACK, PACK)
-        load_round(4)
-        r_codes, r_planes = quantise_banks(transpose_passes(r_sorted, ROUND_PASSES))
-        sort_round(0)
         load_round(5)
         load_state(1)
+        r_codes, r_planes = quantise_banks(transpose_passes(sorted_words(r_sorted), ROUND_PASSES))
+        sort_round(0)
+        load_round(6)
         diffuse(0, r_codes, r_planes)
         transpose_round(0)
         quantise_round(0)
         sort_round(1)
-        load_round(6)
         diffuse(1, r_codes, r_planes)
-        sort_round(2)
 
         for i in range(len(ROUNDS)):
-            if i >= 1 and ROUNDS[i - 1][1] == 1:
-                blend(ROUNDS[i - 1][0])
-            if i + LOAD_AHEAD < len(ROUNDS):
-                load_round(i + LOAD_AHEAD)
-            if i + SORT_AHEAD < len(ROUNDS):
-                sort_round(i + SORT_AHEAD)
             if i + 1 < len(ROUNDS):
                 transpose_round(i + 1)
                 quantise_round(i + 1)
+            if i >= 1 and ROUNDS[i - 1][1] == 1:
+                blend(ROUNDS[i - 1][0])
+            if i + SORT_AHEAD < len(ROUNDS) and ROUNDS[i + SORT_AHEAD][1] == 0:
+                sort_round(i + SORT_AHEAD)
+            if i + LOAD_AHEAD < len(ROUNDS):
+                load_round(i + LOAD_AHEAD)
             passes_of_round(i)
         blend(ROUNDS[-1][0])

@@ -10,11 +10,11 @@ U32 = mybir.dt.uint32
 U8 = mybir.dt.uint8
 FP8X4 = mybir.dt.float8_e4m3fn_x4
 TANH = mybir.ActivationFunctionType.Tanh
+COPY = mybir.ActivationFunctionType.Copy
 
 P = 128
 PACK = 4
 K_PASS = P * PACK
-WORDS_PER_PASS = K_PASS // 2
 
 BATCH = 2
 NODES = 512
@@ -30,9 +30,11 @@ ROUND_COLS = ROUND_PASSES * K_PASS
 SCALE_ROWS = K_PASS // 32
 
 ROUNDS = [(2 * pair + k, half) for pair in range(ROW_BLOCKS // 2) for half in range(2) for k in range(2)]
+ACC_BANKS = 2
+RING_BANKS = 8 - ACC_BANKS
 SORT_AHEAD = 3
 RAW_BUFS = 6
-LOAD_AHEAD = RAW_BUFS + 1
+LOAD_AHEAD = SORT_AHEAD + RAW_BUFS - 1
 
 FLOPS = 2 * (BATCH * SUPPORTS * UNITS * NODES * NODES + BATCH * NODES * (H_CHANNELS + SUPPORTS * UNITS) * UNITS)
 
@@ -65,9 +67,9 @@ def tile_gcrnncell_pb_k_kernel(
         grouped_pool = ctx.enter_context(tc.tile_pool(name="grouped", bufs=3))
         codes_pool = ctx.enter_context(tc.tile_pool(name="codes", bufs=3))
         diffused_pool = ctx.enter_context(tc.tile_pool(name="diffused", bufs=2))
-        blend_pool = ctx.enter_context(tc.tile_pool(name="blend", bufs=2))
-        ring = ctx.enter_context(tc.psum_pool(name="ring", bufs=6))
-        acc_pool = ctx.enter_context(tc.psum_pool(name="acc", bufs=2))
+        blend_pool = ctx.enter_context(tc.tile_pool(name="blend", bufs=3))
+        ring = ctx.enter_context(tc.psum_pool(name="ring", bufs=RING_BANKS))
+        acc_pool = ctx.enter_context(tc.psum_pool(name="acc", bufs=ACC_BANKS))
         ctx.enter_context(tc.manual_schedule())
 
         ident_f32 = keep.tile([P, P], F32)
@@ -88,6 +90,7 @@ def tile_gcrnncell_pb_k_kernel(
         prev_bank_of = {}
         operand_of = {}
         prev_of = {}
+        terms_of = {}
         acc_of = {}
 
         def h_passes_of(half):
@@ -113,7 +116,7 @@ def tile_gcrnncell_pb_k_kernel(
 
         def sort_round(i):
             srt = sorted_pool.tile([P, ROUND_PASSES, 2, P], F32)
-            sort_words(raw_of[i], srt, 0, ROUND_PASSES)
+            sort_words(raw_of[i], srt, 0, h_passes_of(ROUNDS[i][1]))
             sorted_of[i] = srt
 
         def transpose_passes(words_of, n_passes):
@@ -129,16 +132,9 @@ def tile_gcrnncell_pb_k_kernel(
         def sorted_words(srt):
             return lambda g, parity: srt[:, g, parity, :]
 
-        def every_second_word(raw):
-            words = raw[:].bitcast(F32)
-            return lambda g, parity: words[:, g * WORDS_PER_PASS + parity : (g + 1) * WORDS_PER_PASS : 2]
-
         def transpose_round(i):
             row_block, half = ROUNDS[i]
-            if half == 0:
-                banks_of[i] = transpose_passes(sorted_words(sorted_of[i]), ROUND_PASSES)
-            else:
-                banks_of[i] = transpose_passes(every_second_word(raw_of[i]), H_PASSES - ROUND_PASSES)
+            banks_of[i] = transpose_passes(sorted_words(sorted_of[i]), h_passes_of(half))
             if half == 1:
                 b, node_block = divmod(row_block, BLOCKS_PER_BATCH)
                 prev_bank = ring.tile([P, UNITS], BF16, tag="ring")
@@ -195,23 +191,28 @@ def tile_gcrnncell_pb_k_kernel(
                 for s in range(SUPPORTS):
                     kernel_pass(acc, cs_codes[:, s, row_block, :], cs_planes[:, s, row_block, :], H_PASSES + s)
 
+        def prepare_blend(row_block):
+            carried = blend_pool.tile([P, UNITS], F32)
+            nc.vector.tensor_mul(out=carried[:], in0=prev_of[row_block][:], in1=u_sb[:, row_block, :])
+            share = blend_pool.tile([P, UNITS], F32)
+            nc.scalar.activation(out=share[:], in_=u_sb[:, row_block, :], func=COPY, bias=1.0, scale=-1.0)
+            terms_of[row_block] = (carried, share)
+
         def blend(row_block):
+            carried, share = terms_of[row_block]
             cand = blend_pool.tile([P, UNITS], F32)
-            nc.scalar.activation(out=cand[:], in_=acc_of[row_block][:], func=TANH)
-            prev = prev_of[row_block]
-            diff = blend_pool.tile([P, UNITS], F32)
             z = blend_pool.tile([P, UNITS], F32)
             halves = (slice(0, UNITS // 2), slice(UNITS // 2, UNITS))
             for cols in halves:
-                nc.vector.tensor_sub(out=diff[:, cols], in0=prev[:, cols], in1=cand[:, cols])
+                nc.scalar.activation(out=cand[:, cols], in_=acc_of[row_block][:, cols], func=TANH)
             for cols in halves:
-                nc.vector.tensor_mul(out=diff[:, cols], in0=diff[:, cols], in1=u_sb[:, row_block, cols])
+                nc.vector.tensor_mul(out=cand[:, cols], in0=cand[:, cols], in1=share[:, cols])
             for cols in halves:
-                nc.vector.tensor_add(out=z[:, cols], in0=diff[:, cols], in1=cand[:, cols])
+                nc.vector.tensor_add(out=z[:, cols], in0=cand[:, cols], in1=carried[:, cols])
             nc.sync.dma_start(out=out_rows[row_block * P : (row_block + 1) * P, :], in_=z[:])
 
-        def diffuse(b, r_codes, r_planes):
-            for s in range(SUPPORTS):
+        def diffuse(s, r_codes, r_planes):
+            for b in range(BATCH):
                 diffused = diffused_pool.tile([P, BLOCKS_PER_BATCH, P, PACK], BF16, align_bytes=64)
                 for node_block in range(BLOCKS_PER_BATCH):
                     nodes = slice(node_block * P, (node_block + 1) * P)
@@ -227,7 +228,7 @@ def tile_gcrnncell_pb_k_kernel(
                             stop=True,
                         )
                     by_unit = bank[:].rearrange("p t m -> p m t")
-                    if node_block % 2 == 0:
+                    if node_block < BLOCKS_PER_BATCH - 1:
                         nc.scalar.copy(out=diffused[:, node_block], in_=by_unit)
                     else:
                         nc.vector.tensor_copy(out=diffused[:, node_block], in_=by_unit)
@@ -243,6 +244,13 @@ def tile_gcrnncell_pb_k_kernel(
                 out=kernel_words[:, first : first + count, :].bitcast(I32),
                 in_=c_kernel_words[first : first + count].rearrange("g p n t -> p g (n t)").bitcast(I32),
             )
+
+        def load_support_scales(s):
+            for r in range(4):
+                nc.sync.dma_start(
+                    out=sup_planes[r:P:32, s, :].bitcast(I32),
+                    in_=support_scales[s][0, r:SCALE_ROWS:4, :].bitcast(I32),
+                )
 
         def load_state(b):
             nc.sync.dma_start(out=state_sb[:, b], in_=state[b].rearrange("(c p n) -> p c n", p=P, n=NODES))
@@ -265,52 +273,52 @@ def tile_gcrnncell_pb_k_kernel(
                 out=sup_words[:, s, :].bitcast(I32),
                 in_=support_words[s][0].rearrange("p n t -> p (n t)").bitcast(I32),
             )
-        for s in range(SUPPORTS):
-            for r in range(4):
-                nc.sync.dma_start(
-                    out=sup_planes[r:P:32, s, :].bitcast(I32),
-                    in_=support_scales[s][0, r:SCALE_ROWS:4, :].bitcast(I32),
-                )
+        load_support_scales(0)
         load_round(0)
         load_round(1)
+        load_support_scales(1)
+        load_kernel_words(0, 4)
+        load_kernel_words(4, 4)
         for r in range(4):
             nc.sync.dma_start(
                 out=kernel_planes[r:P:32, :, :].bitcast(I32),
                 in_=c_kernel_scales[:, r:SCALE_ROWS:4, :].rearrange("g q n -> q g n").bitcast(I32),
             )
-        load_kernel_words(0, 4)
-        load_kernel_words(4, 4)
         load_round(2)
         load_state(0)
         load_round(3)
         load_kernel_words(8, 4)
         load_kernel_words(12, 4)
-        nc.sync.dma_start(out=u_sb[:], in_=u_rows.rearrange("(r p) k -> p r k", p=P))
         load_round(4)
+        nc.sync.dma_start(out=u_sb[:], in_=u_rows.rearrange("(r p) k -> p r k", p=P))
 
         r_sorted = sorted_pool.tile([P, ROUND_PASSES, 2, P], F32, tag="srt")
         for b in range(BATCH):
             sort_words(r_raw, r_sorted, b * PACK, PACK)
         load_round(5)
-        load_state(1)
         r_codes, r_planes = quantise_banks(transpose_passes(sorted_words(r_sorted), ROUND_PASSES))
         sort_round(0)
         load_round(6)
+        load_state(1)
         diffuse(0, r_codes, r_planes)
+        sort_round(1)
+        load_round(7)
         transpose_round(0)
         quantise_round(0)
-        sort_round(1)
         diffuse(1, r_codes, r_planes)
+        sort_round(2)
 
         for i in range(len(ROUNDS)):
+            if i + SORT_AHEAD < len(ROUNDS):
+                sort_round(i + SORT_AHEAD)
+            if i + LOAD_AHEAD < len(ROUNDS):
+                load_round(i + LOAD_AHEAD)
             if i + 1 < len(ROUNDS):
                 transpose_round(i + 1)
                 quantise_round(i + 1)
             if i >= 1 and ROUNDS[i - 1][1] == 1:
                 blend(ROUNDS[i - 1][0])
-            if i + SORT_AHEAD < len(ROUNDS) and ROUNDS[i + SORT_AHEAD][1] == 0:
-                sort_round(i + SORT_AHEAD)
-            if i + LOAD_AHEAD < len(ROUNDS):
-                load_round(i + LOAD_AHEAD)
+            if ROUNDS[i][1] == 1:
+                prepare_blend(ROUNDS[i][0])
             passes_of_round(i)
         blend(ROUNDS[-1][0])

@@ -29,8 +29,14 @@ ROUND_PASSES = 8
 ROUND_COLS = ROUND_PASSES * K_PASS
 SCALE_ROWS = K_PASS // 32
 
-ROUNDS = [(2 * pair + k, half) for pair in range(ROW_BLOCKS // 2) for half in range(2) for k in range(2)]
-ACC_BANKS = 2
+GROUP = 3
+ROUNDS = [
+    (row_block, half)
+    for first in range(0, ROW_BLOCKS, GROUP)
+    for half in range(2)
+    for row_block in range(first, min(first + GROUP, ROW_BLOCKS))
+]
+ACC_BANKS = GROUP
 RING_BANKS = 8 - ACC_BANKS
 SORT_AHEAD = 3
 RAW_BUFS = 6
@@ -76,7 +82,7 @@ def tile_gcrnncell_pb_k_kernel(
         ident_bf16 = keep.tile([P, P], BF16)
         table_warmer = keep.tile([P, 1], F32)
         kernel_words = keep.tile([P, ALL_PASSES, UNITS], U32, align_bytes=64)
-        kernel_planes = keep.tile([P, ALL_PASSES, UNITS], U8, align_bytes=64)
+        kernel_planes = keep.tile([P, ALL_PASSES // 4, UNITS], U8, align_bytes=64)
         sup_words = keep.tile([P, SUPPORTS, NODES], U32, align_bytes=64)
         sup_planes = keep.tile([P, SUPPORTS, NODES], U8, align_bytes=64)
         cs_codes = keep.tile([P, SUPPORTS, ROW_BLOCKS, P], U32, align_bytes=64)
@@ -173,7 +179,7 @@ def tile_gcrnncell_pb_k_kernel(
                 lhsT=codes.bitcast(FP8X4),
                 lhsT_scale=planes,
                 rhs=kernel_words[:, g, :].bitcast(FP8X4),
-                rhs_scale=kernel_planes[:, g, :],
+                rhs_scale=kernel_planes[4 * (g % 4) : P, g // 4, :],
                 start=(g == 0),
                 stop=(g == ALL_PASSES - 1),
             )
@@ -239,11 +245,19 @@ def tile_gcrnncell_pb_k_kernel(
                     in_=diffused[:].rearrange("p r m t -> p (r m t)"),
                 )
 
-        def load_kernel_words(first, count):
+        def load_kernel_words(slot):
+            four = slice(4 * slot, 4 * slot + 4)
             nc.sync.dma_start(
-                out=kernel_words[:, first : first + count, :].bitcast(I32),
-                in_=c_kernel_words[first : first + count].rearrange("g p n t -> p g (n t)").bitcast(I32),
+                out=kernel_words[:, four, :].bitcast(I32),
+                in_=c_kernel_words[four].rearrange("g p n t -> p g (n t)").bitcast(I32),
             )
+
+        def load_kernel_scales(slot):
+            for quadrant in range(4):
+                nc.sync.dma_start(
+                    out=kernel_planes[32 * quadrant : 32 * quadrant + 16, slot, :].bitcast(I32),
+                    in_=c_kernel_scales[4 * slot : 4 * slot + 4, 4 * quadrant : 4 * quadrant + 4, :].bitcast(I32),
+                )
 
         def load_support_scales(s):
             for r in range(4):
@@ -277,19 +291,18 @@ def tile_gcrnncell_pb_k_kernel(
         load_round(0)
         load_round(1)
         load_support_scales(1)
-        load_kernel_words(0, 4)
-        load_kernel_words(4, 4)
-        for r in range(4):
-            nc.sync.dma_start(
-                out=kernel_planes[r:P:32, :, :].bitcast(I32),
-                in_=c_kernel_scales[:, r:SCALE_ROWS:4, :].rearrange("g q n -> q g n").bitcast(I32),
-            )
+        load_kernel_words(0)
+        load_kernel_scales(0)
+        load_kernel_words(1)
+        load_kernel_scales(1)
         load_round(2)
-        load_state(0)
         load_round(3)
-        load_kernel_words(8, 4)
-        load_kernel_words(12, 4)
+        load_state(0)
+        load_kernel_scales(2)
         load_round(4)
+        load_kernel_words(2)
+        load_kernel_scales(3)
+        load_kernel_words(3)
         nc.sync.dma_start(out=u_sb[:], in_=u_rows.rearrange("(r p) k -> p r k", p=P))
 
         r_sorted = sorted_pool.tile([P, ROUND_PASSES, 2, P], F32, tag="srt")

@@ -29,17 +29,16 @@ ROUND_PASSES = 8
 ROUND_COLS = ROUND_PASSES * K_PASS
 SCALE_ROWS = K_PASS // 32
 
-GROUP = 3
-ROUNDS = [
-    (row_block, half)
-    for first in range(0, ROW_BLOCKS, GROUP)
-    for half in range(2)
-    for row_block in range(first, min(first + GROUP, ROW_BLOCKS))
-]
-ACC_BANKS = GROUP
+LEAD = 3
+ROUNDS = sorted(
+    ((row_block, half) for row_block in range(ROW_BLOCKS) for half in range(2)),
+    key=lambda work: (work[0] + LEAD * work[1], -work[1]),
+)
+ACC_BANKS = LEAD
 RING_BANKS = 8 - ACC_BANKS
 SORT_AHEAD = 3
 RAW_BUFS = 6
+HALVES = (slice(0, UNITS // 2), slice(UNITS // 2, UNITS))
 LOAD_AHEAD = SORT_AHEAD + RAW_BUFS - 1
 
 FLOPS = 2 * (BATCH * SUPPORTS * UNITS * NODES * NODES + BATCH * NODES * (H_CHANNELS + SUPPORTS * UNITS) * UNITS)
@@ -97,6 +96,7 @@ def tile_gcrnncell_pb_k_kernel(
         operand_of = {}
         prev_of = {}
         terms_of = {}
+        cand_of = {}
         acc_of = {}
 
         def h_passes_of(half):
@@ -204,16 +204,19 @@ def tile_gcrnncell_pb_k_kernel(
             nc.scalar.activation(out=share[:], in_=u_sb[:, row_block, :], func=COPY, bias=1.0, scale=-1.0)
             terms_of[row_block] = (carried, share)
 
+        def candidate(row_block):
+            cand = blend_pool.tile([P, UNITS], F32)
+            for cols in HALVES:
+                nc.scalar.activation(out=cand[:, cols], in_=acc_of[row_block][:, cols], func=TANH)
+            cand_of[row_block] = cand
+
         def blend(row_block):
             carried, share = terms_of[row_block]
-            cand = blend_pool.tile([P, UNITS], F32)
+            cand = cand_of[row_block]
             z = blend_pool.tile([P, UNITS], F32)
-            halves = (slice(0, UNITS // 2), slice(UNITS // 2, UNITS))
-            for cols in halves:
-                nc.scalar.activation(out=cand[:, cols], in_=acc_of[row_block][:, cols], func=TANH)
-            for cols in halves:
+            for cols in HALVES:
                 nc.vector.tensor_mul(out=cand[:, cols], in0=cand[:, cols], in1=share[:, cols])
-            for cols in halves:
+            for cols in HALVES:
                 nc.vector.tensor_add(out=z[:, cols], in0=cand[:, cols], in1=carried[:, cols])
             nc.sync.dma_start(out=out_rows[row_block * P : (row_block + 1) * P, :], in_=z[:])
 
@@ -322,6 +325,9 @@ def tile_gcrnncell_pb_k_kernel(
         sort_round(2)
 
         for i in range(len(ROUNDS)):
+            second_before = i >= 1 and ROUNDS[i - 1][1] == 1
+            if second_before:
+                candidate(ROUNDS[i - 1][0])
             if i + SORT_AHEAD < len(ROUNDS):
                 sort_round(i + SORT_AHEAD)
             if i + LOAD_AHEAD < len(ROUNDS):
@@ -329,9 +335,10 @@ def tile_gcrnncell_pb_k_kernel(
             if i + 1 < len(ROUNDS):
                 transpose_round(i + 1)
                 quantise_round(i + 1)
-            if i >= 1 and ROUNDS[i - 1][1] == 1:
+            if second_before:
                 blend(ROUNDS[i - 1][0])
             if ROUNDS[i][1] == 1:
                 prepare_blend(ROUNDS[i][0])
             passes_of_round(i)
+        candidate(ROUNDS[-1][0])
         blend(ROUNDS[-1][0])

@@ -10,7 +10,7 @@ U32 = mybir.dt.uint32
 U8 = mybir.dt.uint8
 FP8X4 = mybir.dt.float8_e4m3fn_x4
 TANH = mybir.ActivationFunctionType.Tanh
-COPY = mybir.ActivationFunctionType.Copy
+ALU = mybir.AluOpType
 
 P = 128
 PACK = 4
@@ -28,20 +28,28 @@ ALL_PASSES = H_PASSES + SUPPORTS
 ROUND_PASSES = 8
 ROUND_COLS = ROUND_PASSES * K_PASS
 SCALE_ROWS = K_PASS // 32
-
-LEAD = 3
-ROUNDS = sorted(
-    ((row_block, half) for row_block in range(ROW_BLOCKS) for half in range(2)),
-    key=lambda work: (work[0] + LEAD * work[1], -work[1]),
-)
-ACC_BANKS = LEAD
-RING_BANKS = 8 - ACC_BANKS
-SORT_AHEAD = 3
+PSUM_BANKS = 8
 RAW_BUFS = 6
+
+SPLIT_BLOCKS = 3
+RUNS = [[(row_block, half)] for half in range(2) for row_block in range(SPLIT_BLOCKS)] + [
+    [(row_block, 0), (row_block, 1)] for row_block in range(SPLIT_BLOCKS, ROW_BLOCKS)
+]
+ROUNDS = [work for run in RUNS for work in run]
+RUNS_AT = [[ROUNDS.index(work) for work in run] for run in RUNS]
+
 HALVES = (slice(0, UNITS // 2), slice(UNITS // 2, UNITS))
-LOAD_AHEAD = SORT_AHEAD + RAW_BUFS - 1
 
 FLOPS = 2 * (BATCH * SUPPORTS * UNITS * NODES * NODES + BATCH * NODES * (H_CHANNELS + SUPPORTS * UNITS) * UNITS)
+
+
+def h_passes_of(half):
+    return ROUND_PASSES if half == 0 else H_PASSES - ROUND_PASSES
+
+
+def place_of(row_block):
+    batch, block = divmod(row_block, BLOCKS_PER_BATCH)
+    return (batch,) + divmod(block, 2)
 
 
 def tile_gcrnncell_pb_k_kernel(
@@ -59,31 +67,30 @@ def tile_gcrnncell_pb_k_kernel(
     out,
 ):
     nc = tc.nc
-    h_rows = h_diff.flatten_outer_dims()
-    u_rows = u.flatten_outer_dims()
-    out_rows = out.rearrange("b (n k) -> (b n) k", k=UNITS)
+    h_rows = h_diff.rearrange("b (h w e) c -> b h e w c", w=P, e=2)
+    out_rows = out.rearrange("b (h w e k) -> b h e w k", w=P, e=2, k=UNITS)
     support_words = (support0_words, support1_words)
     support_scales = (support0_scales, support1_scales)
 
     with ExitStack() as ctx:
         keep = ctx.enter_context(tc.tile_pool(name="keep", bufs=1))
         raw_pool = ctx.enter_context(tc.tile_pool(name="raw", bufs=RAW_BUFS))
-        sorted_pool = ctx.enter_context(tc.tile_pool(name="sorted", bufs=3))
+        sorted_pool = ctx.enter_context(tc.tile_pool(name="sorted", bufs=4))
         grouped_pool = ctx.enter_context(tc.tile_pool(name="grouped", bufs=3))
-        codes_pool = ctx.enter_context(tc.tile_pool(name="codes", bufs=3))
+        codes_pool = ctx.enter_context(tc.tile_pool(name="codes", bufs=5))
         diffused_pool = ctx.enter_context(tc.tile_pool(name="diffused", bufs=2))
         blend_pool = ctx.enter_context(tc.tile_pool(name="blend", bufs=3))
-        ring = ctx.enter_context(tc.psum_pool(name="ring", bufs=RING_BANKS))
-        acc_pool = ctx.enter_context(tc.psum_pool(name="acc", bufs=ACC_BANKS))
+        psum = ctx.enter_context(tc.psum_pool(name="psum", bufs=1))
         ctx.enter_context(tc.manual_schedule())
 
-        ident_f32 = keep.tile([P, P], F32)
-        ident_bf16 = keep.tile([P, P], BF16)
+        ident = keep.tile([P, P], F32)
         table_warmer = keep.tile([P, 1], F32)
         kernel_words = keep.tile([P, ALL_PASSES, UNITS], U32, align_bytes=64)
         kernel_planes = keep.tile([P, ALL_PASSES // 4, UNITS], U8, align_bytes=64)
         sup_words = keep.tile([P, SUPPORTS, NODES], U32, align_bytes=64)
         sup_planes = keep.tile([P, SUPPORTS, NODES], U8, align_bytes=64)
+        r_codes = keep.tile([P, BATCH * PACK, P], U32, align_bytes=64)
+        r_planes = keep.tile([P, BATCH * PACK, P], U8, align_bytes=64)
         cs_codes = keep.tile([P, SUPPORTS, ROW_BLOCKS, P], U32, align_bytes=64)
         cs_planes = keep.tile([P, SUPPORTS, ROW_BLOCKS, P], U8, align_bytes=64)
         u_sb = keep.tile([P, ROW_BLOCKS, UNITS], BF16)
@@ -92,24 +99,34 @@ def tile_gcrnncell_pb_k_kernel(
         raw_of = {}
         sorted_of = {}
         banks_of = {}
-        prev_bank_of = {}
         operand_of = {}
-        prev_of = {}
-        terms_of = {}
+        carried_of = {}
         cand_of = {}
-        acc_of = {}
+        sums_of = {}
+        diffused_of = {}
 
-        def h_passes_of(half):
-            return ROUND_PASSES if half == 0 else H_PASSES - ROUND_PASSES
+        free_banks = list(range(PSUM_BANKS))
+        place_of_bank = {}
+
+        def take_bank(key, shape):
+            place = free_banks[0]
+            free_banks.remove(place)
+            bank = psum.tile(shape, F32, tag="bank%d" % place, name="bank%d" % place)
+            place_of_bank[key] = place
+            return bank
+
+        def give_back(key):
+            free_banks.append(place_of_bank[key])
 
         def load_round(i):
             row_block, half = ROUNDS[i]
+            b, node_half, parity = place_of(row_block)
             width = h_passes_of(half) * K_PASS
             first = half * ROUND_COLS
-            raw = raw_pool.tile([P, ROUND_COLS], BF16)
+            raw = raw_pool.tile([P, ROUND_COLS], BF16, tag="raw")
             nc.sync.dma_start(
                 out=raw[:, :width],
-                in_=h_rows[row_block * P : (row_block + 1) * P, first : first + width],
+                in_=h_rows[b, node_half, parity, :, first : first + width],
             )
             raw_of[i] = raw
 
@@ -120,133 +137,165 @@ def tile_gcrnncell_pb_k_kernel(
                 in_=words.rearrange("p (g j e) -> p g e j", j=P, e=2),
             )
 
-        def sort_round(i):
-            srt = sorted_pool.tile([P, ROUND_PASSES, 2, P], F32)
-            sort_words(raw_of[i], srt, 0, h_passes_of(ROUNDS[i][1]))
-            sorted_of[i] = srt
+        def sort_passes(i, first_pass, n_passes):
+            if first_pass == 0:
+                srt = sorted_pool.tile([P, ROUND_PASSES, 2, P], F32, tag="srt")
+                sorted_of[i] = srt
+            sort_words(raw_of[i], sorted_of[i], first_pass, n_passes)
+            if first_pass + n_passes == h_passes_of(ROUNDS[i][1]) and i + RAW_BUFS < len(ROUNDS):
+                load_round(i + RAW_BUFS)
 
-        def transpose_passes(words_of, n_passes):
+        def sort_round(i):
+            sort_passes(i, 0, h_passes_of(ROUNDS[i][1]))
+
+        def transpose_passes(key, srt, n_passes):
             banks = []
             for pair in range(n_passes // 2):
-                bank = ring.tile([P, 2, 2, P], F32, tag="ring")
+                bank = take_bank((key, pair), [P, 2, 2, P])
                 for g in range(2):
                     for parity in range(2):
-                        nc.tensor.transpose(bank[:, g, parity, :], words_of(2 * pair + g, parity), ident_f32[:])
+                        nc.tensor.transpose(bank[:, g, parity, :], srt[:, 2 * pair + g, parity, :], ident[:])
                 banks.append(bank)
-            return banks
-
-        def sorted_words(srt):
-            return lambda g, parity: srt[:, g, parity, :]
+            banks_of[key] = banks
 
         def transpose_round(i):
-            row_block, half = ROUNDS[i]
-            banks_of[i] = transpose_passes(sorted_words(sorted_of[i]), h_passes_of(half))
-            if half == 1:
-                b, node_block = divmod(row_block, BLOCKS_PER_BATCH)
-                prev_bank = ring.tile([P, UNITS], BF16, tag="ring")
-                for unit_block in range(UNITS // P):
-                    nc.tensor.transpose(
-                        prev_bank[:, unit_block * P : (unit_block + 1) * P],
-                        state_sb[:, b, unit_block, node_block * P : (node_block + 1) * P],
-                        ident_bf16[:],
-                    )
-                prev_bank_of[i] = prev_bank
+            transpose_passes(i, sorted_of[i], h_passes_of(ROUNDS[i][1]))
 
-        def quantise_banks(banks):
-            grouped = grouped_pool.tile([P, ROUND_PASSES, P, PACK], BF16, align_bytes=64)
+        def quantise_pair(key, pair, grouped, codes, planes):
+            two = slice(2 * pair, 2 * pair + 2)
+            nc.scalar.copy(
+                out=grouped[:, two].bitcast(F32), in_=banks_of[key][pair][:].rearrange("p g e r -> p g r e")
+            )
+            give_back((key, pair))
+            nc.vector.quantize_mx(
+                out=codes[:, two, :].rearrange("p g r -> p (g r)").bitcast(FP8X4),
+                scales=planes[:, two, :].rearrange("p g r -> p (g r)"),
+                in_=grouped[:, two].rearrange("p g r t -> p (g r t)"),
+            )
+
+        def quantise_round(i, between):
+            grouped = grouped_pool.tile([P, ROUND_PASSES, P, PACK], BF16, align_bytes=64, tag="grouped")
             codes = codes_pool.tile([P, ROUND_PASSES, P], U32, align_bytes=64)
             planes = codes_pool.tile([P, ROUND_PASSES, P], U8, align_bytes=64)
-            for pair, bank in enumerate(banks):
-                two = slice(2 * pair, 2 * pair + 2)
-                nc.scalar.copy(out=grouped[:, two].bitcast(F32), in_=bank[:].rearrange("p g e r -> p g r e"))
-                nc.vector.quantize_mx(
-                    out=codes[:, two, :].rearrange("p g r -> p (g r)").bitcast(FP8X4),
-                    scales=planes[:, two, :].rearrange("p g r -> p (g r)"),
-                    in_=grouped[:, two].rearrange("p g r t -> p (g r t)"),
-                )
-            return codes, planes
+            for pair in range(len(banks_of[i])):
+                quantise_pair(i, pair, grouped, codes, planes)
+                between()
+            operand_of[i] = (codes, planes)
 
-        def quantise_round(i):
-            operand_of[i] = quantise_banks(banks_of[i])
-            if ROUNDS[i][1] == 1:
-                prev = blend_pool.tile([P, UNITS], BF16)
-                nc.scalar.copy(out=prev[:], in_=prev_bank_of[i][:])
-                prev_of[ROUNDS[i][0]] = prev
-
-        def kernel_pass(acc, codes, planes, g):
+        def kernel_pass(acc, codes, planes, g, cols):
             nc.tensor.matmul_mx(
-                out=acc[:],
+                out=acc,
                 lhsT=codes.bitcast(FP8X4),
                 lhsT_scale=planes,
-                rhs=kernel_words[:, g, :].bitcast(FP8X4),
-                rhs_scale=kernel_planes[4 * (g % 4) : P, g // 4, :],
+                rhs=kernel_words[:, g, cols].bitcast(FP8X4),
+                rhs_scale=kernel_planes[4 * (g % 4) : P, g // 4, cols],
                 start=(g == 0),
                 stop=(g == ALL_PASSES - 1),
             )
 
-        def passes_of_round(i):
+        def passes_of_round(i, acc, cols, after_four):
             row_block, half = ROUNDS[i]
-            if half == 0:
-                acc = acc_pool.tile([P, UNITS], F32)
-                acc_of[row_block] = acc
-            acc = acc_of[row_block]
             codes, planes = operand_of[i]
             for g in range(h_passes_of(half)):
-                kernel_pass(acc, codes[:, g, :], planes[:, g, :], half * ROUND_PASSES + g)
+                kernel_pass(acc, codes[:, g, :], planes[:, g, :], half * ROUND_PASSES + g, cols)
+                if g % 4 == 3:
+                    after_four()
             if half == 1:
                 for s in range(SUPPORTS):
-                    kernel_pass(acc, cs_codes[:, s, row_block, :], cs_planes[:, s, row_block, :], H_PASSES + s)
+                    kernel_pass(
+                        acc, cs_codes[:, s, row_block, :], cs_planes[:, s, row_block, :], H_PASSES + s, cols
+                    )
 
-        def prepare_blend(row_block):
-            carried = blend_pool.tile([P, UNITS], F32)
-            nc.vector.tensor_mul(out=carried[:], in0=prev_of[row_block][:], in1=u_sb[:, row_block, :])
-            share = blend_pool.tile([P, UNITS], F32)
-            nc.scalar.activation(out=share[:], in_=u_sb[:, row_block, :], func=COPY, bias=1.0, scale=-1.0)
-            terms_of[row_block] = (carried, share)
+        def passes_of_run(j, after_four):
+            for i in RUNS_AT[j]:
+                row_block, half = ROUNDS[i]
+                if half == 0:
+                    acc = take_bank(row_block, [P, UNITS])
+                    sums_of[row_block] = acc
+                passes_of_round(i, sums_of[row_block][:], slice(0, UNITS), after_four)
+
+        def transpose_state(pair):
+            b, node_half = divmod(pair, 2)
+            bank = take_bank(("state", pair), [P, UNITS])
+            for unit_block in range(UNITS // P):
+                words = state_sb[:, b, unit_block, node_half * 2 * P : (node_half + 1) * 2 * P].bitcast(F32)
+                nc.tensor.transpose(bank[:, unit_block * P : (unit_block + 1) * P], words, ident[:])
+            banks_of[("state", pair)] = bank
+
+        def prepare_blend(pair):
+            prev = banks_of[("state", pair)][:].bitcast(BF16).rearrange("p (k e) -> p e k", e=2)
+            for parity in range(2):
+                row_block = 2 * pair + parity
+                carried = blend_pool.tile([P, UNITS], F32)
+                nc.vector.tensor_mul(out=carried[:], in0=prev[:, parity, :], in1=u_sb[:, row_block, :])
+                carried_of[row_block] = carried
+            give_back(("state", pair))
 
         def candidate(row_block):
             cand = blend_pool.tile([P, UNITS], F32)
             for cols in HALVES:
-                nc.scalar.activation(out=cand[:, cols], in_=acc_of[row_block][:, cols], func=TANH)
+                nc.scalar.activation(out=cand[:, cols], in_=sums_of[row_block][:, cols], func=TANH)
+            give_back(row_block)
             cand_of[row_block] = cand
 
         def blend(row_block):
-            carried, share = terms_of[row_block]
+            carried = carried_of[row_block]
             cand = cand_of[row_block]
             z = blend_pool.tile([P, UNITS], F32)
             for cols in HALVES:
-                nc.vector.tensor_mul(out=cand[:, cols], in0=cand[:, cols], in1=share[:, cols])
+                nc.vector.scalar_tensor_tensor(
+                    out=cand[:, cols],
+                    in0=u_sb[:, row_block, cols],
+                    scalar=1.0,
+                    in1=cand[:, cols],
+                    op0=ALU.subtract,
+                    op1=ALU.mult,
+                )
             for cols in HALVES:
-                nc.vector.tensor_add(out=z[:, cols], in0=cand[:, cols], in1=carried[:, cols])
-            nc.sync.dma_start(out=out_rows[row_block * P : (row_block + 1) * P, :], in_=z[:])
+                nc.vector.tensor_sub(out=z[:, cols], in0=carried[:, cols], in1=cand[:, cols])
+            b, node_half, parity = place_of(row_block)
+            nc.sync.dma_start(out=out_rows[b, node_half, parity], in_=z[:])
 
-        def diffuse(s, r_codes, r_planes):
-            for b in range(BATCH):
-                diffused = diffused_pool.tile([P, BLOCKS_PER_BATCH, P, PACK], BF16, align_bytes=64)
-                for node_block in range(BLOCKS_PER_BATCH):
-                    nodes = slice(node_block * P, (node_block + 1) * P)
-                    bank = ring.tile([P, PACK, P], F32, tag="ring")
-                    for t in range(PACK):
-                        nc.tensor.matmul_mx(
-                            out=bank[:, t, :],
-                            lhsT=r_codes[:, PACK * b + t, :].bitcast(FP8X4),
-                            lhsT_scale=r_planes[:, PACK * b + t, :],
-                            rhs=sup_words[:, s, nodes].bitcast(FP8X4),
-                            rhs_scale=sup_planes[:, s, nodes],
-                            start=True,
-                            stop=True,
-                        )
-                    by_unit = bank[:].rearrange("p t m -> p m t")
-                    if node_block < BLOCKS_PER_BATCH - 1:
-                        nc.scalar.copy(out=diffused[:, node_block], in_=by_unit)
-                    else:
-                        nc.vector.tensor_copy(out=diffused[:, node_block], in_=by_unit)
+        def diffuse_bank(s, b, node_block):
+            if node_block == 0:
+                fresh = diffused_pool.tile([P, 2, 2, P, PACK], BF16, align_bytes=64, tag="diffused")
+                diffused_of[s, b] = fresh
+            diffused = diffused_of[s, b]
+            nodes = slice(node_block * P, (node_block + 1) * P)
+            bank = take_bank(("diffused", s, b, node_block), [P, PACK, P])
+            for t in range(PACK):
+                nc.tensor.matmul_mx(
+                    out=bank[:, t, :],
+                    lhsT=r_codes[:, PACK * b + t, :].bitcast(FP8X4),
+                    lhsT_scale=r_planes[:, PACK * b + t, :],
+                    rhs=sup_words[:, s, nodes].bitcast(FP8X4),
+                    rhs_scale=sup_planes[:, s, nodes],
+                    start=True,
+                    stop=True,
+                )
+            node_half, quarter = divmod(node_block, 2)
+            w = slice(quarter * (P // 2), (quarter + 1) * (P // 2))
+            by_unit = bank[:].rearrange("p t (w e) -> p e w t", e=2)
+            if node_block % 2 == 0:
+                nc.scalar.copy(out=diffused[:, node_half, :, w, :], in_=by_unit)
+            else:
+                nc.vector.tensor_copy(out=diffused[:, node_half, :, w, :], in_=by_unit)
+            give_back(("diffused", s, b, node_block))
+            if node_block == BLOCKS_PER_BATCH - 1:
                 blocks = slice(b * BLOCKS_PER_BATCH, (b + 1) * BLOCKS_PER_BATCH)
                 nc.vector.quantize_mx(
                     out=cs_codes[:, s, blocks, :].rearrange("p r m -> p (r m)").bitcast(FP8X4),
                     scales=cs_planes[:, s, blocks, :].rearrange("p r m -> p (r m)"),
-                    in_=diffused[:].rearrange("p r m t -> p (r m t)"),
+                    in_=diffused[:].rearrange("p h e w t -> p (h e w t)"),
                 )
+
+        diffusion = [(s, b, n) for b in range(BATCH) for s in range(SUPPORTS) for n in range(BLOCKS_PER_BATCH)]
+
+        def diffuse_next():
+            if diffusion:
+                work = diffusion[0]
+                diffusion.remove(work)
+                diffuse_bank(*work)
 
         def load_kernel_words(slot):
             four = slice(4 * slot, 4 * slot + 4)
@@ -262,12 +311,25 @@ def tile_gcrnncell_pb_k_kernel(
                     in_=c_kernel_scales[4 * slot : 4 * slot + 4, 4 * quadrant : 4 * quadrant + 4, :].bitcast(I32),
                 )
 
+        def load_support_words(s):
+            nc.sync.dma_start(
+                out=sup_words[:, s, :].bitcast(I32),
+                in_=support_words[s][0].rearrange("p n t -> p (n t)").bitcast(I32),
+            )
+
         def load_support_scales(s):
             for r in range(4):
                 nc.sync.dma_start(
                     out=sup_planes[r:P:32, s, :].bitcast(I32),
                     in_=support_scales[s][0, r:SCALE_ROWS:4, :].bitcast(I32),
                 )
+
+        def load_update_gate(b):
+            blocks = slice(b * BLOCKS_PER_BATCH, (b + 1) * BLOCKS_PER_BATCH)
+            nc.sync.dma_start(
+                out=u_sb[:, blocks, :].rearrange("p (h e) k -> p h (e k)", e=2),
+                in_=u[b].rearrange("(h w e) k -> w h (e k)", w=P, e=2),
+            )
 
         def load_state(b):
             nc.sync.dma_start(out=state_sb[:, b], in_=state[b].rearrange("(c p n) -> p c n", p=P, n=NODES))
@@ -276,8 +338,7 @@ def tile_gcrnncell_pb_k_kernel(
         nc.vector.memset(kernel_planes[:].rearrange("p g n -> p (g n)").bitcast(I32), 0)
         nc.vector.memset(table_warmer[:], 0.0)
         nc.scalar.activation(out=table_warmer[:], in_=table_warmer[:], func=TANH)
-        make_identity(nc, ident_f32[:])
-        make_identity(nc, ident_bf16[:])
+        make_identity(nc, ident[:])
 
         r_raw = raw_pool.tile([P, ROUND_COLS], BF16, tag="raw")
         for b in range(BATCH):
@@ -285,60 +346,79 @@ def tile_gcrnncell_pb_k_kernel(
                 out=r_raw[:, b * PACK * NODES : (b + 1) * PACK * NODES],
                 in_=r_prev[b].rearrange("(p t) n -> p (t n)", t=PACK),
             )
-        for s in range(SUPPORTS):
-            nc.sync.dma_start(
-                out=sup_words[:, s, :].bitcast(I32),
-                in_=support_words[s][0].rearrange("p n t -> p (n t)").bitcast(I32),
-            )
+        load_support_words(0)
         load_support_scales(0)
         load_round(0)
-        load_round(1)
+        load_support_words(1)
         load_support_scales(1)
+        load_round(1)
         load_kernel_words(0)
         load_kernel_scales(0)
         load_kernel_words(1)
         load_kernel_scales(1)
         load_round(2)
         load_round(3)
-        load_state(0)
-        load_kernel_scales(2)
-        load_round(4)
         load_kernel_words(2)
-        load_kernel_scales(3)
+        load_kernel_scales(2)
         load_kernel_words(3)
-        nc.sync.dma_start(out=u_sb[:], in_=u_rows.rearrange("(r p) k -> p r k", p=P))
+        load_kernel_scales(3)
+        load_round(4)
+        load_state(0)
 
         r_sorted = sorted_pool.tile([P, ROUND_PASSES, 2, P], F32, tag="srt")
         for b in range(BATCH):
             sort_words(r_raw, r_sorted, b * PACK, PACK)
-        load_round(5)
-        r_codes, r_planes = quantise_banks(transpose_passes(sorted_words(r_sorted), ROUND_PASSES))
+        load_round(RAW_BUFS - 1)
+        load_update_gate(0)
+        transpose_passes("r", r_sorted, ROUND_PASSES)
+        r_grouped = grouped_pool.tile([P, ROUND_PASSES, P, PACK], BF16, align_bytes=64, tag="grouped")
+        for pair in range(ROUND_PASSES // 2):
+            quantise_pair("r", pair, r_grouped, r_codes, r_planes)
         sort_round(0)
-        load_round(6)
-        load_state(1)
-        diffuse(0, r_codes, r_planes)
-        sort_round(1)
-        load_round(7)
+        for node_block in range(BLOCKS_PER_BATCH):
+            diffuse_next()
         transpose_round(0)
-        quantise_round(0)
-        diffuse(1, r_codes, r_planes)
-        sort_round(2)
+        quantise_round(0, lambda: None)
+        sort_round(1)
+        diffuse_next()
+        diffuse_next()
 
-        for i in range(len(ROUNDS)):
-            second_before = i >= 1 and ROUNDS[i - 1][1] == 1
-            if second_before:
-                candidate(ROUNDS[i - 1][0])
-            if i + SORT_AHEAD < len(ROUNDS):
-                sort_round(i + SORT_AHEAD)
-            if i + LOAD_AHEAD < len(ROUNDS):
-                load_round(i + LOAD_AHEAD)
-            if i + 1 < len(ROUNDS):
-                transpose_round(i + 1)
-                quantise_round(i + 1)
-            if second_before:
-                blend(ROUNDS[i - 1][0])
-            if ROUNDS[i][1] == 1:
-                prepare_blend(ROUNDS[i][0])
-            passes_of_round(i)
-        candidate(ROUNDS[-1][0])
-        blend(ROUNDS[-1][0])
+        for j in range(len(RUNS)):
+            finished = [row_block for row_block, half in RUNS[j - 1] if half == 1] if j > 0 else []
+            following = RUNS_AT[j + 1] if j + 1 < len(RUNS) else []
+            to_sort = [
+                (i, first_pass)
+                for i in (RUNS_AT[j + 2] if j + 2 < len(RUNS) else [])
+                for first_pass in range(0, h_passes_of(ROUNDS[i][1]), 2)
+            ]
+
+            def sort_next():
+                if to_sort:
+                    i, first_pass = to_sort[0]
+                    to_sort.remove((i, first_pass))
+                    sort_passes(i, first_pass, 2)
+
+            for row_block in finished:
+                candidate(row_block)
+            for i in following:
+                transpose_round(i)
+            for row_block in finished:
+                if row_block % 2 == 0:
+                    transpose_state(row_block // 2)
+            steady = len(following) > 1
+            for i in following:
+                quantise_round(i, sort_next if steady else (lambda: None))
+            for row_block in finished:
+                if row_block % 2 == 0:
+                    prepare_blend(row_block // 2)
+                blend(row_block)
+            for left in range(len(to_sort)):
+                sort_next()
+            if j == 2:
+                load_state(1)
+                load_update_gate(1)
+            passes_of_run(j, diffuse_next)
+        for row_block, half in RUNS[-1]:
+            if half == 1:
+                candidate(row_block)
+                blend(row_block)

@@ -29,6 +29,11 @@ ROUND_PASSES = 8
 ROUND_COLS = ROUND_PASSES * K_PASS
 SCALE_ROWS = K_PASS // 32
 PSUM_BANKS = 8
+DIFFUSED_ON_VECTOR = [(0, 0), (1, 0)]
+SCALAR_SORTS_FROM = 6
+SORTS_FIRST = 4
+BLENDS_FROM = 6
+STATE_STEPS = [1, 5]
 RAW_BUFS = 6
 
 SPLIT_BLOCKS = 3
@@ -77,7 +82,7 @@ def tile_gcrnncell_pb_k_kernel(
         raw_pool = ctx.enter_context(tc.tile_pool(name="raw", bufs=RAW_BUFS))
         sorted_pool = ctx.enter_context(tc.tile_pool(name="sorted", bufs=4))
         grouped_pool = ctx.enter_context(tc.tile_pool(name="grouped", bufs=3))
-        codes_pool = ctx.enter_context(tc.tile_pool(name="codes", bufs=5))
+        codes_pool = ctx.enter_context(tc.tile_pool(name="codes", bufs=4))
         diffused_pool = ctx.enter_context(tc.tile_pool(name="diffused", bufs=2))
         blend_pool = ctx.enter_context(tc.tile_pool(name="blend", bufs=3))
         psum = ctx.enter_context(tc.psum_pool(name="psum", bufs=1))
@@ -103,7 +108,9 @@ def tile_gcrnncell_pb_k_kernel(
         carried_of = {}
         cand_of = {}
         sums_of = {}
+        prev_of = {}
         diffused_of = {}
+        to_quantise = []
 
         free_banks = list(range(PSUM_BANKS))
         place_of_bank = {}
@@ -118,6 +125,12 @@ def tile_gcrnncell_pb_k_kernel(
         def give_back(key):
             free_banks.append(place_of_bank[key])
 
+        def copy_words(on_vector, out, in_):
+            if on_vector:
+                nc.vector.tensor_copy(out=out, in_=in_)
+            else:
+                nc.scalar.copy(out=out, in_=in_)
+
         def load_round(i):
             row_block, half = ROUNDS[i]
             b, node_half, parity = place_of(row_block)
@@ -130,42 +143,39 @@ def tile_gcrnncell_pb_k_kernel(
             )
             raw_of[i] = raw
 
-        def sort_words(raw, srt, first_pass, n_passes):
+        def sort_words(raw, srt, first_pass, n_passes, on_scalar):
             words = raw[:, first_pass * K_PASS : (first_pass + n_passes) * K_PASS].bitcast(F32)
-            nc.vector.tensor_copy(
-                out=srt[:, first_pass : first_pass + n_passes],
-                in_=words.rearrange("p (g j e) -> p g e j", j=P, e=2),
+            copy_words(
+                not on_scalar,
+                srt[:, first_pass : first_pass + n_passes],
+                words.rearrange("p (g j e) -> p g e j", j=P, e=2),
             )
 
-        def sort_passes(i, first_pass, n_passes):
-            if first_pass == 0:
+        def sort_passes(i, first_pass, n_passes, on_scalar):
+            if i not in sorted_of:
                 srt = sorted_pool.tile([P, ROUND_PASSES, 2, P], F32, tag="srt")
                 sorted_of[i] = srt
-            sort_words(raw_of[i], sorted_of[i], first_pass, n_passes)
-            if first_pass + n_passes == h_passes_of(ROUNDS[i][1]) and i + RAW_BUFS < len(ROUNDS):
-                load_round(i + RAW_BUFS)
+            sort_words(raw_of[i], sorted_of[i], first_pass, n_passes, on_scalar)
 
         def sort_round(i):
-            sort_passes(i, 0, h_passes_of(ROUNDS[i][1]))
+            sort_passes(i, 0, h_passes_of(ROUNDS[i][1]), False)
 
-        def transpose_passes(key, srt, n_passes):
+        def transpose_passes(key, srt, first_pass, n_passes):
             banks = []
             for pair in range(n_passes // 2):
                 bank = take_bank((key, pair), [P, 2, 2, P])
                 for g in range(2):
                     for parity in range(2):
-                        nc.tensor.transpose(bank[:, g, parity, :], srt[:, 2 * pair + g, parity, :], ident[:])
+                        nc.tensor.transpose(bank[:, g, parity, :], srt[:, first_pass + 2 * pair + g, parity, :], ident[:])
                 banks.append(bank)
             banks_of[key] = banks
 
         def transpose_round(i):
-            transpose_passes(i, sorted_of[i], h_passes_of(ROUNDS[i][1]))
+            transpose_passes(i, sorted_of[i], 0, h_passes_of(ROUNDS[i][1]))
 
-        def quantise_pair(key, pair, grouped, codes, planes):
-            two = slice(2 * pair, 2 * pair + 2)
-            nc.scalar.copy(
-                out=grouped[:, two].bitcast(F32), in_=banks_of[key][pair][:].rearrange("p g e r -> p g r e")
-            )
+        def quantise_pair(key, pair, first_pair, on_vector, grouped, codes, planes):
+            two = slice(2 * (first_pair + pair), 2 * (first_pair + pair) + 2)
+            copy_words(on_vector, grouped[:, two].bitcast(F32), banks_of[key][pair][:].rearrange("p g e r -> p g r e"))
             give_back((key, pair))
             nc.vector.quantize_mx(
                 out=codes[:, two, :].rearrange("p g r -> p (g r)").bitcast(FP8X4),
@@ -178,7 +188,7 @@ def tile_gcrnncell_pb_k_kernel(
             codes = codes_pool.tile([P, ROUND_PASSES, P], U32, align_bytes=64)
             planes = codes_pool.tile([P, ROUND_PASSES, P], U8, align_bytes=64)
             for pair in range(len(banks_of[i])):
-                quantise_pair(i, pair, grouped, codes, planes)
+                quantise_pair(i, pair, 0, False, grouped, codes, planes)
                 between()
             operand_of[i] = (codes, planes)
 
@@ -220,19 +230,24 @@ def tile_gcrnncell_pb_k_kernel(
             for unit_block in range(UNITS // P):
                 words = state_sb[:, b, unit_block, node_half * 2 * P : (node_half + 1) * 2 * P].bitcast(F32)
                 nc.tensor.transpose(bank[:, unit_block * P : (unit_block + 1) * P], words, ident[:])
+            prev = blend_pool.tile([P, UNITS], F32, bufs=2)
             banks_of[("state", pair)] = bank
+            prev_of[pair] = prev
+
+        def copy_state(pair):
+            nc.scalar.copy(out=prev_of[pair][:], in_=banks_of[("state", pair)][:])
+            give_back(("state", pair))
 
         def prepare_blend(pair):
-            prev = banks_of[("state", pair)][:].bitcast(BF16).rearrange("p (k e) -> p e k", e=2)
+            prev = prev_of[pair][:].bitcast(BF16).rearrange("p (k e) -> p e k", e=2)
             for parity in range(2):
                 row_block = 2 * pair + parity
                 carried = blend_pool.tile([P, UNITS], F32)
                 nc.vector.tensor_mul(out=carried[:], in0=prev[:, parity, :], in1=u_sb[:, row_block, :])
                 carried_of[row_block] = carried
-            give_back(("state", pair))
 
         def candidate(row_block):
-            cand = blend_pool.tile([P, UNITS], F32)
+            cand = blend_pool.tile([P, UNITS], F32, bufs=4)
             for cols in HALVES:
                 nc.scalar.activation(out=cand[:, cols], in_=sums_of[row_block][:, cols], func=TANH)
             give_back(row_block)
@@ -241,7 +256,7 @@ def tile_gcrnncell_pb_k_kernel(
         def blend(row_block):
             carried = carried_of[row_block]
             cand = cand_of[row_block]
-            z = blend_pool.tile([P, UNITS], F32)
+            z = blend_pool.tile([P, UNITS], F32, bufs=2)
             for cols in HALVES:
                 nc.vector.scalar_tensor_tensor(
                     out=cand[:, cols],
@@ -276,18 +291,23 @@ def tile_gcrnncell_pb_k_kernel(
             node_half, quarter = divmod(node_block, 2)
             w = slice(quarter * (P // 2), (quarter + 1) * (P // 2))
             by_unit = bank[:].rearrange("p t (w e) -> p e w t", e=2)
-            if node_block % 2 == 0:
-                nc.scalar.copy(out=diffused[:, node_half, :, w, :], in_=by_unit)
-            else:
-                nc.vector.tensor_copy(out=diffused[:, node_half, :, w, :], in_=by_unit)
+            copy_words((s, b) in DIFFUSED_ON_VECTOR and node_block % 2 == 1, diffused[:, node_half, :, w, :], by_unit)
             give_back(("diffused", s, b, node_block))
             if node_block == BLOCKS_PER_BATCH - 1:
-                blocks = slice(b * BLOCKS_PER_BATCH, (b + 1) * BLOCKS_PER_BATCH)
-                nc.vector.quantize_mx(
-                    out=cs_codes[:, s, blocks, :].rearrange("p r m -> p (r m)").bitcast(FP8X4),
-                    scales=cs_planes[:, s, blocks, :].rearrange("p r m -> p (r m)"),
-                    in_=diffused[:].rearrange("p h e w t -> p (h e w t)"),
-                )
+                to_quantise.append((s, b))
+
+        def quantise_diffused():
+            for s, b in to_quantise:
+                quantise_part(s, b)
+            to_quantise.clear()
+
+        def quantise_part(s, b):
+            blocks = slice(b * BLOCKS_PER_BATCH, (b + 1) * BLOCKS_PER_BATCH)
+            nc.vector.quantize_mx(
+                out=cs_codes[:, s, blocks, :].rearrange("p r m -> p (r m)").bitcast(FP8X4),
+                scales=cs_planes[:, s, blocks, :].rearrange("p r m -> p (r m)"),
+                in_=diffused_of[s, b][:].rearrange("p h e w t -> p (h e w t)"),
+            )
 
         diffusion = [(s, b, n) for b in range(BATCH) for s in range(SUPPORTS) for n in range(BLOCKS_PER_BATCH)]
 
@@ -296,6 +316,13 @@ def tile_gcrnncell_pb_k_kernel(
                 work = diffusion[0]
                 diffusion.remove(work)
                 diffuse_bank(*work)
+
+        def diffuse_banks(n):
+            for left in range(n):
+                diffuse_next()
+
+        def nothing():
+            return
 
         def load_kernel_words(slot):
             four = slice(4 * slot, 4 * slot + 4)
@@ -341,17 +368,21 @@ def tile_gcrnncell_pb_k_kernel(
         make_identity(nc, ident[:])
 
         r_raw = raw_pool.tile([P, ROUND_COLS], BF16, tag="raw")
-        for b in range(BATCH):
+
+        def load_r(b):
             nc.sync.dma_start(
                 out=r_raw[:, b * PACK * NODES : (b + 1) * PACK * NODES],
                 in_=r_prev[b].rearrange("(p t) n -> p (t n)", t=PACK),
             )
+
+        load_r(0)
         load_support_words(0)
         load_support_scales(0)
         load_round(0)
         load_support_words(1)
         load_support_scales(1)
         load_round(1)
+        load_r(1)
         load_kernel_words(0)
         load_kernel_scales(0)
         load_kernel_words(1)
@@ -363,62 +394,91 @@ def tile_gcrnncell_pb_k_kernel(
         load_kernel_words(3)
         load_kernel_scales(3)
         load_round(4)
-        load_state(0)
 
         r_sorted = sorted_pool.tile([P, ROUND_PASSES, 2, P], F32, tag="srt")
-        for b in range(BATCH):
-            sort_words(r_raw, r_sorted, b * PACK, PACK)
-        load_round(RAW_BUFS - 1)
-        load_update_gate(0)
-        transpose_passes("r", r_sorted, ROUND_PASSES)
         r_grouped = grouped_pool.tile([P, ROUND_PASSES, P, PACK], BF16, align_bytes=64, tag="grouped")
-        for pair in range(ROUND_PASSES // 2):
-            quantise_pair("r", pair, r_grouped, r_codes, r_planes)
-        sort_round(0)
-        for node_block in range(BLOCKS_PER_BATCH):
-            diffuse_next()
-        transpose_round(0)
-        quantise_round(0, lambda: None)
-        sort_round(1)
-        diffuse_next()
-        diffuse_next()
 
+        def sort_r(b):
+            sort_words(r_raw, r_sorted, b * PACK, PACK, False)
+
+        def transpose_r(b):
+            transpose_passes(("r", b), r_sorted, b * PACK, PACK)
+
+        def quantise_r(b):
+            for pair in range(PACK // 2):
+                quantise_pair(("r", b), pair, b * PACK // 2, pair == 1, r_grouped, r_codes, r_planes)
+
+        sort_r(0)
+        transpose_r(0)
+        quantise_r(0)
+        sort_round(0)
+        diffuse_banks(4)
+        transpose_round(0)
+        sort_round(1)
+        sort_r(1)
+        quantise_diffused()
+        quantise_round(0, nothing)
+        transpose_round(1)
+        transpose_r(1)
+        load_round(RAW_BUFS - 1)
+        load_round(RAW_BUFS)
+        load_round(RAW_BUFS + 1)
+
+        to_blend = []
         for j in range(len(RUNS)):
-            finished = [row_block for row_block, half in RUNS[j - 1] if half == 1] if j > 0 else []
             following = RUNS_AT[j + 1] if j + 1 < len(RUNS) else []
-            to_sort = [
-                (i, first_pass)
-                for i in (RUNS_AT[j + 2] if j + 2 < len(RUNS) else [])
-                for first_pass in range(0, h_passes_of(ROUNDS[i][1]), 2)
-            ]
+            after = RUNS_AT[j + 2] if j + 2 < len(RUNS) else []
+            to_sort = [(i, first_pass) for i in after for first_pass in range(0, h_passes_of(ROUNDS[i][1]), 2)]
+            by_scalar = [work for work in to_sort if j >= SCALAR_SORTS_FROM and work[1] == 2 and ROUNDS[work[0]][1] == 1]
+            by_vector = [work for work in to_sort if work not in by_scalar]
 
             def sort_next():
-                if to_sort:
-                    i, first_pass = to_sort[0]
-                    to_sort.remove((i, first_pass))
-                    sort_passes(i, first_pass, 2)
+                if by_vector:
+                    i, first_pass = by_vector[0]
+                    by_vector.remove((i, first_pass))
+                    sort_passes(i, first_pass, 2, False)
 
-            for row_block in finished:
-                candidate(row_block)
-            for i in following:
-                transpose_round(i)
-            for row_block in finished:
+            for row_block, half in RUNS[j - 1] if j > 0 else []:
+                if half == 1:
+                    candidate(row_block)
+                    to_blend.append(row_block)
+            blends = to_blend[: 2 if not after else 1] if j >= BLENDS_FROM else []
+            if j > 0:
+                for i in following:
+                    transpose_round(i)
+            for row_block in blends:
                 if row_block % 2 == 0:
                     transpose_state(row_block // 2)
-            steady = len(following) > 1
+            if j > 0:
+                for left in range(SORTS_FIRST):
+                    sort_next()
             for i in following:
-                quantise_round(i, sort_next if steady else (lambda: None))
-            for row_block in finished:
+                quantise_round(i, sort_next if j > 0 else nothing)
+            if j == 0:
+                quantise_r(1)
+            quantise_diffused()
+            for i, first_pass in by_scalar:
+                sort_passes(i, first_pass, 2, True)
+            for row_block in blends:
+                if row_block % 2 == 0:
+                    copy_state(row_block // 2)
+            for left in range(len(by_vector)):
+                sort_next()
+            for i in after:
+                if i + RAW_BUFS < len(ROUNDS) and i > 1:
+                    load_round(i + RAW_BUFS)
+            for row_block in blends:
+                to_blend.remove(row_block)
                 if row_block % 2 == 0:
                     prepare_blend(row_block // 2)
                 blend(row_block)
-            for left in range(len(to_sort)):
-                sort_next()
-            if j == 2:
-                load_state(1)
-                load_update_gate(1)
+            if j in STATE_STEPS:
+                load_state(STATE_STEPS.index(j))
+                load_update_gate(STATE_STEPS.index(j))
             passes_of_run(j, diffuse_next)
-        for row_block, half in RUNS[-1]:
-            if half == 1:
+            if j == 0:
+                diffuse_banks(6)
+        for row_block in to_blend + [RUNS[-1][0][0]]:
+            if row_block == RUNS[-1][0][0]:
                 candidate(row_block)
-                blend(row_block)
+            blend(row_block)

@@ -29,10 +29,11 @@ ROUND_PASSES = 8
 ROUND_COLS = ROUND_PASSES * K_PASS
 SCALE_ROWS = K_PASS // 32
 PSUM_BANKS = 8
-DIFFUSED_ON_VECTOR = [(0, 0), (1, 0)]
+DIFFUSED_ON_VECTOR = [(0, 0)]
 SCALAR_SORTS_FROM = 6
 SORTS_FIRST = 4
-BLENDS_FROM = 6
+BLENDS_OF_STEP = [0, 0, 0, 0, 0, 0, 1, 1, 1, 3, 1]
+D_FIRST = 4
 STATE_STEPS = [1, 5]
 RAW_BUFS = 6
 
@@ -221,8 +222,17 @@ def tile_gcrnncell_pb_k_kernel(
                 row_block, half = ROUNDS[i]
                 if half == 0:
                     acc = take_bank(row_block, [P, UNITS])
-                    sums_of[row_block] = acc
-                passes_of_round(i, sums_of[row_block][:], slice(0, UNITS), after_four)
+                    sums_of[row_block] = [acc, acc]
+                passes_of_round(i, sums_of[row_block][0][:], slice(0, UNITS), after_four)
+
+        def passes_by_halves(j):
+            row_block = RUNS[j][0][0]
+            sums_of[row_block] = []
+            for part, cols in enumerate(HALVES):
+                acc = take_bank((row_block, part), [P, UNITS])
+                sums_of[row_block].append(acc)
+                for i in RUNS_AT[j]:
+                    passes_of_round(i, acc[:, cols], cols, nothing)
 
         def transpose_state(pair):
             b, node_half = divmod(pair, 2)
@@ -248,16 +258,49 @@ def tile_gcrnncell_pb_k_kernel(
 
         def candidate(row_block):
             cand = blend_pool.tile([P, UNITS], F32, bufs=4)
-            for cols in HALVES:
-                nc.scalar.activation(out=cand[:, cols], in_=sums_of[row_block][:, cols], func=TANH)
-            give_back(row_block)
             cand_of[row_block] = cand
+            for cols, acc in zip(HALVES, sums_of[row_block]):
+                tanh_of(row_block, acc, cols)
+            give_back(row_block)
+
+        def tanh_of(row_block, acc, cols):
+            nc.scalar.activation(out=cand_of[row_block][:, cols], in_=acc[:, cols], func=TANH)
+
+        def sort_filler(i, first_pass):
+            return lambda: sort_passes(i, first_pass, 2, False)
+
+        def blend_fillers(row_block):
+            return [lambda: scale_candidate(row_block, HALVES), lambda: add_terms(row_block)]
+
+        def add_terms(row_block):
+            z = blend_pool.tile([P, UNITS], F32, bufs=2)
+            subtract_terms(row_block, z, HALVES)
+            store(row_block, z, slice(0, UNITS))
 
         def blend(row_block):
-            carried = carried_of[row_block]
-            cand = cand_of[row_block]
+            for work in blend_fillers(row_block):
+                work()
+
+        def store(row_block, z, cols):
+            b, node_half, parity = place_of(row_block)
+            nc.sync.dma_start(out=out_rows[b, node_half, parity, :, cols], in_=z[:, cols])
+
+        def finish_by_halves(row_block):
+            cand = blend_pool.tile([P, UNITS], F32, bufs=4)
+            cand_of[row_block] = cand
             z = blend_pool.tile([P, UNITS], F32, bufs=2)
-            for cols in HALVES:
+            for part, cols in enumerate(HALVES):
+                middle = (cols.start + cols.stop) // 2
+                quarters = (slice(cols.start, middle), slice(middle, cols.stop))
+                for quarter in quarters:
+                    tanh_of(row_block, sums_of[row_block][part], quarter)
+                scale_candidate(row_block, quarters)
+                subtract_terms(row_block, z, quarters)
+                store(row_block, z, cols)
+
+        def scale_candidate(row_block, pieces):
+            cand = cand_of[row_block]
+            for cols in pieces:
                 nc.vector.scalar_tensor_tensor(
                     out=cand[:, cols],
                     in0=u_sb[:, row_block, cols],
@@ -266,10 +309,12 @@ def tile_gcrnncell_pb_k_kernel(
                     op0=ALU.subtract,
                     op1=ALU.mult,
                 )
-            for cols in HALVES:
-                nc.vector.tensor_sub(out=z[:, cols], in0=carried[:, cols], in1=cand[:, cols])
-            b, node_half, parity = place_of(row_block)
-            nc.sync.dma_start(out=out_rows[b, node_half, parity], in_=z[:])
+
+        def subtract_terms(row_block, z, pieces):
+            for cols in pieces:
+                nc.vector.tensor_sub(
+                    out=z[:, cols], in0=carried_of[row_block][:, cols], in1=cand_of[row_block][:, cols]
+                )
 
         def diffuse_bank(s, b, node_block):
             if node_block == 0:
@@ -428,42 +473,45 @@ def tile_gcrnncell_pb_k_kernel(
         for j in range(len(RUNS)):
             following = RUNS_AT[j + 1] if j + 1 < len(RUNS) else []
             after = RUNS_AT[j + 2] if j + 2 < len(RUNS) else []
-            to_sort = [(i, first_pass) for i in after for first_pass in range(0, h_passes_of(ROUNDS[i][1]), 2)]
-            by_scalar = [work for work in to_sort if j >= SCALAR_SORTS_FROM and work[1] == 2 and ROUNDS[work[0]][1] == 1]
-            by_vector = [work for work in to_sort if work not in by_scalar]
-
-            def sort_next():
-                if by_vector:
-                    i, first_pass = by_vector[0]
-                    by_vector.remove((i, first_pass))
-                    sort_passes(i, first_pass, 2, False)
-
             for row_block, half in RUNS[j - 1] if j > 0 else []:
                 if half == 1:
                     candidate(row_block)
                     to_blend.append(row_block)
-            blends = to_blend[: 2 if not after else 1] if j >= BLENDS_FROM else []
+            blends = to_blend[: BLENDS_OF_STEP[j]]
+            states = [row_block // 2 for row_block in blends if row_block % 2 == 0]
+
+            to_sort = [(i, first_pass) for i in after for first_pass in range(0, h_passes_of(ROUNDS[i][1]), 2)]
+            by_scalar = [work for work in to_sort if j >= SCALAR_SORTS_FROM and work in ((after[-1], 2),)]
+            fillers = [sort_filler(*work) for work in to_sort if work not in by_scalar]
+            done_early = [row_block for row_block in blends[:1] if not after and row_block % 2 == 1]
+            for row_block in done_early:
+                fillers.extend(blend_fillers(row_block))
+
+            def fill():
+                if fillers:
+                    work = fillers[0]
+                    fillers.remove(work)
+                    work()
+
             if j > 0:
                 for i in following:
                     transpose_round(i)
-            for row_block in blends:
-                if row_block % 2 == 0:
-                    transpose_state(row_block // 2)
-            if j > 0:
+            for pair in states:
+                transpose_state(pair)
+            if j > 0 and after:
                 for left in range(SORTS_FIRST):
-                    sort_next()
+                    fill()
             for i in following:
-                quantise_round(i, sort_next if j > 0 else nothing)
+                quantise_round(i, fill if j > 0 else nothing)
             if j == 0:
                 quantise_r(1)
             quantise_diffused()
+            for pair in states:
+                copy_state(pair)
             for i, first_pass in by_scalar:
                 sort_passes(i, first_pass, 2, True)
-            for row_block in blends:
-                if row_block % 2 == 0:
-                    copy_state(row_block // 2)
-            for left in range(len(by_vector)):
-                sort_next()
+            for left in range(len(fillers)):
+                fill()
             for i in after:
                 if i + RAW_BUFS < len(ROUNDS) and i > 1:
                     load_round(i + RAW_BUFS)
@@ -471,14 +519,15 @@ def tile_gcrnncell_pb_k_kernel(
                 to_blend.remove(row_block)
                 if row_block % 2 == 0:
                     prepare_blend(row_block // 2)
-                blend(row_block)
+                if row_block not in done_early:
+                    blend(row_block)
             if j in STATE_STEPS:
                 load_state(STATE_STEPS.index(j))
                 load_update_gate(STATE_STEPS.index(j))
-            passes_of_run(j, diffuse_next)
+            if j < len(RUNS) - 1:
+                passes_of_run(j, diffuse_next)
+            else:
+                passes_by_halves(j)
             if j == 0:
-                diffuse_banks(6)
-        for row_block in to_blend + [RUNS[-1][0][0]]:
-            if row_block == RUNS[-1][0][0]:
-                candidate(row_block)
-            blend(row_block)
+                diffuse_banks(D_FIRST)
+        finish_by_halves(RUNS[-1][0][0])

@@ -34,6 +34,9 @@ SCALAR_SORTS_FROM = 6
 SORTS_FIRST = 4
 BLENDS_OF_STEP = [0, 0, 0, 0, 0, 0, 1, 1, 1, 3, 1]
 D_FIRST = 4
+STATES_FROM = 6
+QUANT_BANKS = 2
+SORT_PASSES = 4
 STATE_STEPS = [1, 5]
 RAW_BUFS = 6
 
@@ -174,22 +177,27 @@ def tile_gcrnncell_pb_k_kernel(
         def transpose_round(i):
             transpose_passes(i, sorted_of[i], 0, h_passes_of(ROUNDS[i][1]))
 
-        def quantise_pair(key, pair, first_pair, on_vector, grouped, codes, planes):
+        def copy_bank(key, pair, first_pair, on_vector, grouped):
             two = slice(2 * (first_pair + pair), 2 * (first_pair + pair) + 2)
             copy_words(on_vector, grouped[:, two].bitcast(F32), banks_of[key][pair][:].rearrange("p g e r -> p g r e"))
             give_back((key, pair))
+
+        def quantise_passes(passes, grouped, codes, planes):
             nc.vector.quantize_mx(
-                out=codes[:, two, :].rearrange("p g r -> p (g r)").bitcast(FP8X4),
-                scales=planes[:, two, :].rearrange("p g r -> p (g r)"),
-                in_=grouped[:, two].rearrange("p g r t -> p (g r t)"),
+                out=codes[:, passes, :].rearrange("p g r -> p (g r)").bitcast(FP8X4),
+                scales=planes[:, passes, :].rearrange("p g r -> p (g r)"),
+                in_=grouped[:, passes].rearrange("p g r t -> p (g r t)"),
             )
 
         def quantise_round(i, between):
             grouped = grouped_pool.tile([P, ROUND_PASSES, P, PACK], BF16, align_bytes=64, tag="grouped")
             codes = codes_pool.tile([P, ROUND_PASSES, P], U32, align_bytes=64)
             planes = codes_pool.tile([P, ROUND_PASSES, P], U8, align_bytes=64)
-            for pair in range(len(banks_of[i])):
-                quantise_pair(i, pair, 0, False, grouped, codes, planes)
+            for first in range(0, len(banks_of[i]), QUANT_BANKS):
+                last = min(first + QUANT_BANKS, len(banks_of[i]))
+                for pair in range(first, last):
+                    copy_bank(i, pair, 0, False, grouped)
+                quantise_passes(slice(2 * first, 2 * last), grouped, codes, planes)
                 between()
             operand_of[i] = (codes, planes)
 
@@ -266,8 +274,8 @@ def tile_gcrnncell_pb_k_kernel(
         def tanh_of(row_block, acc, cols):
             nc.scalar.activation(out=cand_of[row_block][:, cols], in_=acc[:, cols], func=TANH)
 
-        def sort_filler(i, first_pass):
-            return lambda: sort_passes(i, first_pass, 2, False)
+        def sort_filler(i, first_pass, n_passes):
+            return lambda: sort_passes(i, first_pass, n_passes, False)
 
         def blend_fillers(row_block):
             return [lambda: scale_candidate(row_block, HALVES), lambda: add_terms(row_block)]
@@ -451,7 +459,9 @@ def tile_gcrnncell_pb_k_kernel(
 
         def quantise_r(b):
             for pair in range(PACK // 2):
-                quantise_pair(("r", b), pair, b * PACK // 2, pair == 1, r_grouped, r_codes, r_planes)
+                copy_bank(("r", b), pair, b * PACK // 2, pair == 1, r_grouped)
+                passes = slice(b * PACK + 2 * pair, b * PACK + 2 * pair + 2)
+                quantise_passes(passes, r_grouped, r_codes, r_planes)
 
         sort_r(0)
         transpose_r(0)
@@ -478,10 +488,14 @@ def tile_gcrnncell_pb_k_kernel(
                     candidate(row_block)
                     to_blend.append(row_block)
             blends = to_blend[: BLENDS_OF_STEP[j]]
-            states = [row_block // 2 for row_block in blends if row_block % 2 == 0]
+            states = [j - STATES_FROM] if 0 <= j - STATES_FROM < ROW_BLOCKS // 2 else []
 
-            to_sort = [(i, first_pass) for i in after for first_pass in range(0, h_passes_of(ROUNDS[i][1]), 2)]
-            by_scalar = [work for work in to_sort if j >= SCALAR_SORTS_FROM and work in ((after[-1], 2),)]
+            to_sort = [
+                (i, first, min(SORT_PASSES, h_passes_of(ROUNDS[i][1]) - first))
+                for i in after
+                for first in range(0, h_passes_of(ROUNDS[i][1]), SORT_PASSES)
+            ]
+            by_scalar = [work for work in to_sort if j >= SCALAR_SORTS_FROM and work[2] == 2][:1]
             fillers = [sort_filler(*work) for work in to_sort if work not in by_scalar]
             done_early = [row_block for row_block in blends[:1] if not after and row_block % 2 == 1]
             for row_block in done_early:
@@ -508,8 +522,8 @@ def tile_gcrnncell_pb_k_kernel(
             quantise_diffused()
             for pair in states:
                 copy_state(pair)
-            for i, first_pass in by_scalar:
-                sort_passes(i, first_pass, 2, True)
+            for work in by_scalar:
+                sort_passes(*work, True)
             for left in range(len(fillers)):
                 fill()
             for i in after:

from contextlib import ExitStack

import concourse.mybir as mybir
from concourse.masks import make_identity

F32 = mybir.dt.float32
BF16 = mybir.dt.bfloat16
I32 = mybir.dt.int32
U32 = mybir.dt.uint32
U8 = mybir.dt.uint8
FP8X4 = mybir.dt.float8_e4m3fn_x4
TANH = mybir.ActivationFunctionType.Tanh
ALU = mybir.AluOpType

P = 128
PACK = 4
K_PASS = P * PACK

BATCH = 2
NODES = 512
UNITS = 512
SUPPORTS = 2
H_CHANNELS = 7168
BLOCKS_PER_BATCH = NODES // P
ROW_BLOCKS = BATCH * BLOCKS_PER_BATCH
H_PASSES = H_CHANNELS // K_PASS
ALL_PASSES = H_PASSES + SUPPORTS
ROUND_PASSES = 8
ROUND_COLS = ROUND_PASSES * K_PASS
SCALE_ROWS = K_PASS // 32
PSUM_BANKS = 8
DIFFUSED_ON_VECTOR = [(0, 0)]
SCALAR_SORTS_FROM = 6
SORTS_FIRST = 4
BLENDS_OF_STEP = [0, 0, 0, 0, 0, 0, 1, 1, 1, 3, 1]
D_FIRST = 4
STATES_FROM = 6
QUANT_BANKS = 2
SORT_PASSES = 4
STATE_STEPS = [1, 5]
RAW_BUFS = 6

SPLIT_BLOCKS = 3
RUNS = [[(row_block, half)] for half in range(2) for row_block in range(SPLIT_BLOCKS)] + [
    [(row_block, 0), (row_block, 1)] for row_block in range(SPLIT_BLOCKS, ROW_BLOCKS)
]
ROUNDS = [work for run in RUNS for work in run]
RUNS_AT = [[ROUNDS.index(work) for work in run] for run in RUNS]

HALVES = (slice(0, UNITS // 2), slice(UNITS // 2, UNITS))

FLOPS = 2 * (BATCH * SUPPORTS * UNITS * NODES * NODES + BATCH * NODES * (H_CHANNELS + SUPPORTS * UNITS) * UNITS)


def h_passes_of(half):
    return ROUND_PASSES if half == 0 else H_PASSES - ROUND_PASSES


def place_of(row_block):
    batch, block = divmod(row_block, BLOCKS_PER_BATCH)
    return (batch,) + divmod(block, 2)


def tile_gcrnncell_pb_k_kernel(
    tc,
    r_prev,
    h_diff,
    u,
    state,
    support0_words,
    support0_scales,
    support1_words,
    support1_scales,
    c_kernel_words,
    c_kernel_scales,
    out,
):
    nc = tc.nc
    h_rows = h_diff.rearrange("b (h w e) c -> b h e w c", w=P, e=2)
    out_rows = out.rearrange("b (h w e k) -> b h e w k", w=P, e=2, k=UNITS)
    support_words = (support0_words, support1_words)
    support_scales = (support0_scales, support1_scales)

    with ExitStack() as ctx:
        keep = ctx.enter_context(tc.tile_pool(name="keep", bufs=1))
        raw_pool = ctx.enter_context(tc.tile_pool(name="raw", bufs=RAW_BUFS))
        sorted_pool = ctx.enter_context(tc.tile_pool(name="sorted", bufs=4))
        grouped_pool = ctx.enter_context(tc.tile_pool(name="grouped", bufs=3))
        codes_pool = ctx.enter_context(tc.tile_pool(name="codes", bufs=4))
        diffused_pool = ctx.enter_context(tc.tile_pool(name="diffused", bufs=2))
        blend_pool = ctx.enter_context(tc.tile_pool(name="blend", bufs=3))
        psum = ctx.enter_context(tc.psum_pool(name="psum", bufs=1))
        ctx.enter_context(tc.manual_schedule())

        ident = keep.tile([P, P], F32)
        table_warmer = keep.tile([P, 1], F32)
        kernel_words = keep.tile([P, ALL_PASSES, UNITS], U32, align_bytes=64)
        kernel_planes = keep.tile([P, ALL_PASSES // 4, UNITS], U8, align_bytes=64)
        sup_words = keep.tile([P, SUPPORTS, NODES], U32, align_bytes=64)
        sup_planes = keep.tile([P, SUPPORTS, NODES], U8, align_bytes=64)
        r_codes = keep.tile([P, BATCH * PACK, P], U32, align_bytes=64)
        r_planes = keep.tile([P, BATCH * PACK, P], U8, align_bytes=64)
        cs_codes = keep.tile([P, SUPPORTS, ROW_BLOCKS, P], U32, align_bytes=64)
        cs_planes = keep.tile([P, SUPPORTS, ROW_BLOCKS, P], U8, align_bytes=64)
        u_sb = keep.tile([P, ROW_BLOCKS, UNITS], BF16)
        state_sb = keep.tile([P, BATCH, UNITS // P, NODES], BF16)

        raw_of = {}
        sorted_of = {}
        banks_of = {}
        operand_of = {}
        carried_of = {}
        cand_of = {}
        sums_of = {}
        prev_of = {}
        diffused_of = {}
        to_quantise = []

        free_banks = list(range(PSUM_BANKS))
        place_of_bank = {}

        def take_bank(key, shape):
            place = free_banks[0]
            free_banks.remove(place)
            bank = psum.tile(shape, F32, tag="bank%d" % place, name="bank%d" % place)
            place_of_bank[key] = place
            return bank

        def give_back(key):
            free_banks.append(place_of_bank[key])

        def copy_words(on_vector, out, in_):
            if on_vector:
                nc.vector.tensor_copy(out=out, in_=in_)
            else:
                nc.scalar.copy(out=out, in_=in_)

        def load_round(i):
            row_block, half = ROUNDS[i]
            b, node_half, parity = place_of(row_block)
            width = h_passes_of(half) * K_PASS
            first = half * ROUND_COLS
            raw = raw_pool.tile([P, ROUND_COLS], BF16, tag="raw")
            nc.sync.dma_start(
                out=raw[:, :width],
                in_=h_rows[b, node_half, parity, :, first : first + width],
            )
            raw_of[i] = raw

        def sort_words(raw, srt, first_pass, n_passes, on_scalar):
            words = raw[:, first_pass * K_PASS : (first_pass + n_passes) * K_PASS].bitcast(F32)
            copy_words(
                not on_scalar,
                srt[:, first_pass : first_pass + n_passes],
                words.rearrange("p (g j e) -> p g e j", j=P, e=2),
            )

        def sort_passes(i, first_pass, n_passes, on_scalar):
            if i not in sorted_of:
                srt = sorted_pool.tile([P, ROUND_PASSES, 2, P], F32, tag="srt")
                sorted_of[i] = srt
            sort_words(raw_of[i], sorted_of[i], first_pass, n_passes, on_scalar)

        def sort_round(i):
            sort_passes(i, 0, h_passes_of(ROUNDS[i][1]), False)

        def transpose_passes(key, srt, first_pass, n_passes):
            banks = []
            for pair in range(n_passes // 2):
                bank = take_bank((key, pair), [P, 2, 2, P])
                for g in range(2):
                    for parity in range(2):
                        nc.tensor.transpose(bank[:, g, parity, :], srt[:, first_pass + 2 * pair + g, parity, :], ident[:])
                banks.append(bank)
            banks_of[key] = banks

        def transpose_round(i):
            transpose_passes(i, sorted_of[i], 0, h_passes_of(ROUNDS[i][1]))

        def copy_bank(key, pair, first_pair, on_vector, grouped):
            two = slice(2 * (first_pair + pair), 2 * (first_pair + pair) + 2)
            copy_words(on_vector, grouped[:, two].bitcast(F32), banks_of[key][pair][:].rearrange("p g e r -> p g r e"))
            give_back((key, pair))

        def quantise_passes(passes, grouped, codes, planes):
            nc.vector.quantize_mx(
                out=codes[:, passes, :].rearrange("p g r -> p (g r)").bitcast(FP8X4),
                scales=planes[:, passes, :].rearrange("p g r -> p (g r)"),
                in_=grouped[:, passes].rearrange("p g r t -> p (g r t)"),
            )

        def quantise_round(i, between):
            grouped = grouped_pool.tile([P, ROUND_PASSES, P, PACK], BF16, align_bytes=64, tag="grouped")
            codes = codes_pool.tile([P, ROUND_PASSES, P], U32, align_bytes=64)
            planes = codes_pool.tile([P, ROUND_PASSES, P], U8, align_bytes=64)
            for first in range(0, len(banks_of[i]), QUANT_BANKS):
                last = min(first + QUANT_BANKS, len(banks_of[i]))
                for pair in range(first, last):
                    copy_bank(i, pair, 0, False, grouped)
                quantise_passes(slice(2 * first, 2 * last), grouped, codes, planes)
                between()
            operand_of[i] = (codes, planes)

        def kernel_pass(acc, codes, planes, g, cols):
            nc.tensor.matmul_mx(
                out=acc,
                lhsT=codes.bitcast(FP8X4),
                lhsT_scale=planes,
                rhs=kernel_words[:, g, cols].bitcast(FP8X4),
                rhs_scale=kernel_planes[4 * (g % 4) : P, g // 4, cols],
                start=(g == 0),
                stop=(g == ALL_PASSES - 1),
            )

        def passes_of_round(i, acc, cols, after_four):
            row_block, half = ROUNDS[i]
            codes, planes = operand_of[i]
            for g in range(h_passes_of(half)):
                kernel_pass(acc, codes[:, g, :], planes[:, g, :], half * ROUND_PASSES + g, cols)
                if g % 4 == 3:
                    after_four()
            if half == 1:
                for s in range(SUPPORTS):
                    kernel_pass(
                        acc, cs_codes[:, s, row_block, :], cs_planes[:, s, row_block, :], H_PASSES + s, cols
                    )

        def passes_of_run(j, after_four):
            for i in RUNS_AT[j]:
                row_block, half = ROUNDS[i]
                if half == 0:
                    acc = take_bank(row_block, [P, UNITS])
                    sums_of[row_block] = [acc, acc]
                passes_of_round(i, sums_of[row_block][0][:], slice(0, UNITS), after_four)

        def passes_by_halves(j):
            row_block = RUNS[j][0][0]
            sums_of[row_block] = []
            for part, cols in enumerate(HALVES):
                acc = take_bank((row_block, part), [P, UNITS])
                sums_of[row_block].append(acc)
                for i in RUNS_AT[j]:
                    passes_of_round(i, acc[:, cols], cols, nothing)

        def transpose_state(pair):
            b, node_half = divmod(pair, 2)
            bank = take_bank(("state", pair), [P, UNITS])
            for unit_block in range(UNITS // P):
                words = state_sb[:, b, unit_block, node_half * 2 * P : (node_half + 1) * 2 * P].bitcast(F32)
                nc.tensor.transpose(bank[:, unit_block * P : (unit_block + 1) * P], words, ident[:])
            prev = blend_pool.tile([P, UNITS], F32, bufs=2)
            banks_of[("state", pair)] = bank
            prev_of[pair] = prev

        def copy_state(pair):
            nc.scalar.copy(out=prev_of[pair][:], in_=banks_of[("state", pair)][:])
            give_back(("state", pair))

        def prepare_blend(pair):
            prev = prev_of[pair][:].bitcast(BF16).rearrange("p (k e) -> p e k", e=2)
            for parity in range(2):
                row_block = 2 * pair + parity
                carried = blend_pool.tile([P, UNITS], F32)
                nc.vector.tensor_mul(out=carried[:], in0=prev[:, parity, :], in1=u_sb[:, row_block, :])
                carried_of[row_block] = carried

        def candidate(row_block):
            cand = blend_pool.tile([P, UNITS], F32, bufs=4)
            cand_of[row_block] = cand
            for cols, acc in zip(HALVES, sums_of[row_block]):
                tanh_of(row_block, acc, cols)
            give_back(row_block)

        def tanh_of(row_block, acc, cols):
            nc.scalar.activation(out=cand_of[row_block][:, cols], in_=acc[:, cols], func=TANH)

        def sort_filler(i, first_pass, n_passes):
            return lambda: sort_passes(i, first_pass, n_passes, False)

        def blend_fillers(row_block):
            return [lambda: scale_candidate(row_block, HALVES), lambda: add_terms(row_block)]

        def add_terms(row_block):
            z = blend_pool.tile([P, UNITS], F32, bufs=2)
            subtract_terms(row_block, z, HALVES)
            store(row_block, z, slice(0, UNITS))

        def blend(row_block):
            for work in blend_fillers(row_block):
                work()

        def store(row_block, z, cols):
            b, node_half, parity = place_of(row_block)
            nc.sync.dma_start(out=out_rows[b, node_half, parity, :, cols], in_=z[:, cols])

        def finish_by_halves(row_block):
            cand = blend_pool.tile([P, UNITS], F32, bufs=4)
            cand_of[row_block] = cand
            z = blend_pool.tile([P, UNITS], F32, bufs=2)
            for part, cols in enumerate(HALVES):
                middle = (cols.start + cols.stop) // 2
                quarters = (slice(cols.start, middle), slice(middle, cols.stop))
                for quarter in quarters:
                    tanh_of(row_block, sums_of[row_block][part], quarter)
                scale_candidate(row_block, quarters)
                subtract_terms(row_block, z, quarters)
                store(row_block, z, cols)

        def scale_candidate(row_block, pieces):
            cand = cand_of[row_block]
            for cols in pieces:
                nc.vector.scalar_tensor_tensor(
                    out=cand[:, cols],
                    in0=u_sb[:, row_block, cols],
                    scalar=1.0,
                    in1=cand[:, cols],
                    op0=ALU.subtract,
                    op1=ALU.mult,
                )

        def subtract_terms(row_block, z, pieces):
            for cols in pieces:
                nc.vector.tensor_sub(
                    out=z[:, cols], in0=carried_of[row_block][:, cols], in1=cand_of[row_block][:, cols]
                )

        def diffuse_bank(s, b, node_block):
            if node_block == 0:
                fresh = diffused_pool.tile([P, 2, 2, P, PACK], BF16, align_bytes=64, tag="diffused")
                diffused_of[s, b] = fresh
            diffused = diffused_of[s, b]
            nodes = slice(node_block * P, (node_block + 1) * P)
            bank = take_bank(("diffused", s, b, node_block), [P, PACK, P])
            for t in range(PACK):
                nc.tensor.matmul_mx(
                    out=bank[:, t, :],
                    lhsT=r_codes[:, PACK * b + t, :].bitcast(FP8X4),
                    lhsT_scale=r_planes[:, PACK * b + t, :],
                    rhs=sup_words[:, s, nodes].bitcast(FP8X4),
                    rhs_scale=sup_planes[:, s, nodes],
                    start=True,
                    stop=True,
                )
            node_half, quarter = divmod(node_block, 2)
            w = slice(quarter * (P // 2), (quarter + 1) * (P // 2))
            by_unit = bank[:].rearrange("p t (w e) -> p e w t", e=2)
            copy_words((s, b) in DIFFUSED_ON_VECTOR and node_block % 2 == 1, diffused[:, node_half, :, w, :], by_unit)
            give_back(("diffused", s, b, node_block))
            if node_block == BLOCKS_PER_BATCH - 1:
                to_quantise.append((s, b))

        def quantise_diffused():
            for s, b in to_quantise:
                quantise_part(s, b)
            to_quantise.clear()

        def quantise_part(s, b):
            blocks = slice(b * BLOCKS_PER_BATCH, (b + 1) * BLOCKS_PER_BATCH)
            nc.vector.quantize_mx(
                out=cs_codes[:, s, blocks, :].rearrange("p r m -> p (r m)").bitcast(FP8X4),
                scales=cs_planes[:, s, blocks, :].rearrange("p r m -> p (r m)"),
                in_=diffused_of[s, b][:].rearrange("p h e w t -> p (h e w t)"),
            )

        diffusion = [(s, b, n) for b in range(BATCH) for s in range(SUPPORTS) for n in range(BLOCKS_PER_BATCH)]

        def diffuse_next():
            if diffusion:
                work = diffusion[0]
                diffusion.remove(work)
                diffuse_bank(*work)

        def diffuse_banks(n):
            for left in range(n):
                diffuse_next()

        def nothing():
            return

        def load_kernel_words(slot):
            four = slice(4 * slot, 4 * slot + 4)
            nc.sync.dma_start(
                out=kernel_words[:, four, :].bitcast(I32),
                in_=c_kernel_words[four].rearrange("g p n t -> p g (n t)").bitcast(I32),
            )

        def load_kernel_scales(slot):
            for quadrant in range(4):
                nc.sync.dma_start(
                    out=kernel_planes[32 * quadrant : 32 * quadrant + 16, slot, :].bitcast(I32),
                    in_=c_kernel_scales[4 * slot : 4 * slot + 4, 4 * quadrant : 4 * quadrant + 4, :].bitcast(I32),
                )

        def load_support_words(s):
            nc.sync.dma_start(
                out=sup_words[:, s, :].bitcast(I32),
                in_=support_words[s][0].rearrange("p n t -> p (n t)").bitcast(I32),
            )

        def load_support_scales(s):
            for r in range(4):
                nc.sync.dma_start(
                    out=sup_planes[r:P:32, s, :].bitcast(I32),
                    in_=support_scales[s][0, r:SCALE_ROWS:4, :].bitcast(I32),
                )

        def load_update_gate(b):
            blocks = slice(b * BLOCKS_PER_BATCH, (b + 1) * BLOCKS_PER_BATCH)
            nc.sync.dma_start(
                out=u_sb[:, blocks, :].rearrange("p (h e) k -> p h (e k)", e=2),
                in_=u[b].rearrange("(h w e) k -> w h (e k)", w=P, e=2),
            )

        def load_state(b):
            nc.sync.dma_start(out=state_sb[:, b], in_=state[b].rearrange("(c p n) -> p c n", p=P, n=NODES))

        nc.vector.memset(sup_planes[:].rearrange("p s n -> p (s n)").bitcast(I32), 0)
        nc.vector.memset(kernel_planes[:].rearrange("p g n -> p (g n)").bitcast(I32), 0)
        nc.vector.memset(table_warmer[:], 0.0)
        nc.scalar.activation(out=table_warmer[:], in_=table_warmer[:], func=TANH)
        make_identity(nc, ident[:])

        r_raw = raw_pool.tile([P, ROUND_COLS], BF16, tag="raw")

        def load_r(b):
            nc.sync.dma_start(
                out=r_raw[:, b * PACK * NODES : (b + 1) * PACK * NODES],
                in_=r_prev[b].rearrange("(p t) n -> p (t n)", t=PACK),
            )

        load_r(0)
        load_support_words(0)
        load_support_scales(0)
        load_round(0)
        load_support_words(1)
        load_support_scales(1)
        load_round(1)
        load_r(1)
        load_kernel_words(0)
        load_kernel_scales(0)
        load_kernel_words(1)
        load_kernel_scales(1)
        load_round(2)
        load_round(3)
        load_kernel_words(2)
        load_kernel_scales(2)
        load_kernel_words(3)
        load_kernel_scales(3)
        load_round(4)

        r_sorted = sorted_pool.tile([P, ROUND_PASSES, 2, P], F32, tag="srt")
        r_grouped = grouped_pool.tile([P, ROUND_PASSES, P, PACK], BF16, align_bytes=64, tag="grouped")

        def sort_r(b):
            sort_words(r_raw, r_sorted, b * PACK, PACK, False)

        def transpose_r(b):
            transpose_passes(("r", b), r_sorted, b * PACK, PACK)

        def quantise_r(b):
            for pair in range(PACK // 2):
                copy_bank(("r", b), pair, b * PACK // 2, pair == 1, r_grouped)
                passes = slice(b * PACK + 2 * pair, b * PACK + 2 * pair + 2)
                quantise_passes(passes, r_grouped, r_codes, r_planes)

        sort_r(0)
        transpose_r(0)
        quantise_r(0)
        sort_round(0)
        diffuse_banks(4)
        transpose_round(0)
        sort_round(1)
        sort_r(1)
        quantise_diffused()
        quantise_round(0, nothing)
        transpose_round(1)
        transpose_r(1)
        load_round(RAW_BUFS - 1)
        load_round(RAW_BUFS)
        load_round(RAW_BUFS + 1)

        to_blend = []
        for j in range(len(RUNS)):
            following = RUNS_AT[j + 1] if j + 1 < len(RUNS) else []
            after = RUNS_AT[j + 2] if j + 2 < len(RUNS) else []
            for row_block, half in RUNS[j - 1] if j > 0 else []:
                if half == 1:
                    candidate(row_block)
                    to_blend.append(row_block)
            blends = to_blend[: BLENDS_OF_STEP[j]]
            states = [j - STATES_FROM] if 0 <= j - STATES_FROM < ROW_BLOCKS // 2 else []

            to_sort = [
                (i, first, min(SORT_PASSES, h_passes_of(ROUNDS[i][1]) - first))
                for i in after
                for first in range(0, h_passes_of(ROUNDS[i][1]), SORT_PASSES)
            ]
            by_scalar = [work for work in to_sort if j >= SCALAR_SORTS_FROM and work[2] == 2][:1]
            fillers = [sort_filler(*work) for work in to_sort if work not in by_scalar]
            done_early = [row_block for row_block in blends[:1] if not after and row_block % 2 == 1]
            for row_block in done_early:
                fillers.extend(blend_fillers(row_block))

            def fill():
                if fillers:
                    work = fillers[0]
                    fillers.remove(work)
                    work()

            if j > 0:
                for i in following:
                    transpose_round(i)
            for pair in states:
                transpose_state(pair)
            if j > 0 and after:
                for left in range(SORTS_FIRST):
                    fill()
            for i in following:
                quantise_round(i, fill if j > 0 else nothing)
            if j == 0:
                quantise_r(1)
            quantise_diffused()
            for pair in states:
                copy_state(pair)
            for work in by_scalar:
                sort_passes(*work, True)
            for left in range(len(fillers)):
                fill()
            for i in after:
                if i + RAW_BUFS < len(ROUNDS) and i > 1:
                    load_round(i + RAW_BUFS)
            for row_block in blends:
                to_blend.remove(row_block)
                if row_block % 2 == 0:
                    prepare_blend(row_block // 2)
                if row_block not in done_early:
                    blend(row_block)
            if j in STATE_STEPS:
                load_state(STATE_STEPS.index(j))
                load_update_gate(STATE_STEPS.index(j))
            if j < len(RUNS) - 1:
                passes_of_run(j, diffuse_next)
            else:
                passes_by_halves(j)
            if j == 0:
                diffuse_banks(D_FIRST)
        finish_by_halves(RUNS[-1][0][0])
